import numpy as np
import ml_dtypes


def mxq(x, axis, fmt="e4m3"):
    dtype, down = {"e4m3": (ml_dtypes.float8_e4m3fn, 7), "e5m2": (ml_dtypes.float8_e5m2, 14)}[fmt]
    v = np.moveaxis(np.asarray(x, np.float32).astype(ml_dtypes.bfloat16).astype(np.float64), axis, -1)
    blocks = v.reshape(v.shape[:-1] + (-1, 32))
    amax = np.abs(blocks).max(-1, keepdims=True)
    byte = np.maximum(np.where(amax > 0, np.frexp(amax)[1] - 1 + 127, 0) - down, 1)
    scale = np.exp2(byte - 127.0)
    codes = (blocks / scale).astype(np.float32).astype(dtype).astype(np.float64)
    return np.moveaxis((codes * scale).reshape(v.shape), -1, axis)


WIDE = False


def mx_kscale(k):
    if not WIDE:
        return np.ones(k)
    levels = np.array([10, -10, 5, -5, 0])
    a = np.random.permutation(np.resize(levels, k // 512 * 4)).reshape(k // 512, 4)
    idx = np.arange(k)
    return np.exp2(a[idx // 512, idx % 128 // 32])


BF16 = ml_dtypes.bfloat16


def bf(x):
    return np.asarray(x, np.float32).astype(BF16)


def f64(x):
    return np.asarray(x).astype(np.float64)


B, C, H, W = 4, 2560, 8, 12
C5 = C // 5
P = H * W
STEP = 1
EPS_BN = 1e-5
ERF_TERMS = 120


def erf(v):
    u = np.clip(v, -6.0, 6.0)
    u2 = 2.0 * u * u
    term = u
    total = u
    for n in range(1, ERF_TERMS):
        term = term * (u2 / (2.0 * n + 1.0))
        total = total + term
    return 2.0 / np.sqrt(np.pi) * np.exp(-u * u) * total


def gelu(v):
    return 0.5 * v * (1.0 + erf(v / np.sqrt(2.0)))


def bn(v, g, b, m, var):
    scale = g / np.sqrt(var + EPS_BN)
    return v * scale[None, :, None, None] + (b - m * scale)[None, :, None, None]


def setup_inputs():
    t = mx_kscale(C)
    d = {"x": bf(np.random.standard_normal((B, C, H, W))),
         "bn1_g": bf(np.random.uniform(0.5, 1.5, C)),
         "bn1_b": bf(np.random.standard_normal(C) * 0.3),
         "bn1_m": bf(np.random.standard_normal(C) * 0.3),
         "bn1_v": bf(np.random.uniform(0.5, 1.5, C))}
    for i, n in enumerate("tbrlc"):
        ti = t[i * C5:(i + 1) * C5]
        d["w" + n] = bf(np.random.standard_normal((C5, C)) / np.sqrt(C) * ti[:, None])
        d["b" + n] = bf(np.random.standard_normal(C5) * 0.3 * ti)
    d["wf1"] = bf(np.random.standard_normal((C, C)) / np.sqrt(C) / t[None, :])
    d["bf1"] = bf(np.random.standard_normal(C) * 0.3)
    return d


def reference(x, bn1_g, bn1_b, bn1_m, bn1_v, wt, bt, wb, bb, wr, br, wl, bl, wc, bc, wf1, bf1):
    h = gelu(bn(f64(x), f64(bn1_g), f64(bn1_b), f64(bn1_m), f64(bn1_v)))
    hq = mxq(h.reshape(B, C, P), 1, "e4m3")
    x_t = ((mxq(f64(wt), 1, "e4m3") @ hq) + f64(bt)[:, None]).reshape(B, C5, H, W)
    x_b = ((mxq(f64(wb), 1, "e4m3") @ hq) + f64(bb)[:, None]).reshape(B, C5, H, W)
    x_r = ((mxq(f64(wr), 1, "e4m3") @ hq) + f64(br)[:, None]).reshape(B, C5, H, W)
    x_l = ((mxq(f64(wl), 1, "e4m3") @ hq) + f64(bl)[:, None]).reshape(B, C5, H, W)
    x_c = ((mxq(f64(wc), 1, "e4m3") @ hq) + f64(bc)[:, None]).reshape(B, C5, H, W)
    x_t = np.pad(x_t, ((0, 0), (0, 0), (0, STEP), (0, 0)))[:, :, 1:1 + H, :]
    x_b = np.pad(x_b, ((0, 0), (0, 0), (STEP, 0), (0, 0)))[:, :, 0:H, :]
    x_l = np.pad(x_l, ((0, 0), (0, 0), (0, 0), (0, STEP)))[:, :, :, 1:1 + W]
    x_r = np.pad(x_r, ((0, 0), (0, 0), (0, 0), (STEP, 0)))[:, :, :, 0:W]
    cat = np.concatenate([x_t, x_b, x_r, x_l, x_c], axis=1)
    lm = (mxq(f64(wf1), 1, "e4m3") @ mxq(cat.reshape(B, C, P), 1, "e4m3")) + f64(bf1)[:, None]
    return lm.reshape(B, C, H, W)

@@ -1,0 +1,322 @@
+from contextlib import ExitStack
+
+import concourse.mybir as mybir
+from concourse.masks import make_identity
+
+F32 = mybir.dt.float32
+BF16 = mybir.dt.bfloat16
+U32 = mybir.dt.uint32
+U8 = mybir.dt.uint8
+FP8X4 = mybir.dt.float8_e4m3fn_x4
+ACT = mybir.ActivationFunctionType
+ALU = mybir.AluOpType
+
+P = 128
+BATCH = 4
+C = 2560
+PIX = 96
+NPIX = BATCH * PIX
+G = 5
+UNITS = 10
+NB = 8
+EPS_BN = 1e-5
+SHIFT = [-12, 12, 1, -1, 0]
+POOL_REGROUP = [0, 1, 2]
+
+FLOPS = 2 * 2 * C * C * NPIX
+
+
+def tile_caterpillarblock_a2_3_np5_pa_kernel(
+    tc, x, bn1_g, bn1_b, bn1_m, bn1_v, wt, bt, wb, bb, wr, br, wl, bl, wc, bc, wf1, bf1, out
+):
+    nc = tc.nc
+    pillars = [wt, wb, wr, wl, wc]
+    xv = x.rearrange("b c i j -> b c (i j)")
+    outv = out.rearrange("b c i j -> b c (i j)")
+
+    with ExitStack() as ctx:
+        const = ctx.enter_context(tc.tile_pool(name="const", bufs=1))
+        rawp = ctx.enter_context(tc.tile_pool(name="rawp", bufs=NB))
+        grpp = ctx.enter_context(tc.tile_pool(name="grpp", bufs=2))
+        codp = ctx.enter_context(tc.tile_pool(name="codp", bufs=3))
+        outp = ctx.enter_context(tc.tile_pool(name="outp", bufs=3))
+        psum = ctx.enter_context(tc.psum_pool(name="psum", bufs=1))
+        ctx.enter_context(tc.manual_schedule())
+
+        ident = const.tile([P, P], F32, name="ident")
+        prw1 = const.tile([P, 256], BF16, name="prw1")
+        prw2 = const.tile([P, 256], BF16, name="prw2")
+        x_sb = const.tile([P, UNITS, BATCH, 2, PIX], BF16, name="x_sb")
+        hpl = const.tile([P, 2 * UNITS, NPIX], BF16, name="hpl")
+        hgrp = const.tile([P, G, NPIX, 4], BF16, name="hgrp", align_bytes=64)
+        hcod = const.tile([P, G, NPIX], U32, name="hcod", align_bytes=64)
+        hscl = const.tile([P, G, NPIX], U8, name="hscl", align_bytes=64)
+        cgrp = const.tile([P, G, NPIX, 4], BF16, name="cgrp", align_bytes=64)
+        ccod = const.tile([P, G, NPIX], U32, name="ccod", align_bytes=64)
+        cscl = const.tile([P, G, NPIX], U8, name="cscl", align_bytes=64)
+
+        make_identity(nc, ident[:])
+        nc.vector.memset(prw1[:], 0.0)
+        nc.vector.memset(prw2[:], 0.0)
+
+        for r, vec in enumerate([bn1_g, bn1_b, bn1_m, bn1_v]):
+            nc.scalar.dma_start(
+                out=prw1[10 * r : 10 * r + 10, :], in_=vec.rearrange("(r c) -> r c", c=256)
+            )
+
+        raws = {}
+
+        def unit_rows(n):
+            if n < UNITS:
+                return pillars[n // 2][256 * (n % 2) : 256 * (n % 2) + 256, :]
+            return wf1[256 * (n - UNITS) : 256 * (n - UNITS) + 256, :]
+
+        def new_raw(n):
+            raws[n] = rawp.tile([P, 2 * C], BF16, name="wraw", tag="wraw")
+
+        def load_half(n, e):
+            nc.sync.dma_start(
+                out=raws[n][:, e * C : (e + 1) * C],
+                in_=unit_rows(n).rearrange("(p e) c -> p e c", e=2)[:, e, :],
+            )
+
+        def load_unit(n):
+            new_raw(n)
+            nc.sync.dma_start(out=raws[n][:], in_=unit_rows(n).rearrange("(p e) c -> p (e c)", e=2))
+
+        def load_x(u):
+            nc.sync.dma_start(
+                out=x_sb[:, u, :, :, :].rearrange("p b e q -> p b (e q)"),
+                in_=xv[:, 256 * u : 256 * u + 256, :].rearrange("b (p e) q -> p b (e q)", e=2),
+            )
+
+        new_raw(0)
+        load_half(0, 0)
+        for u in range(8):
+            load_x(u)
+        load_half(0, 1)
+        for u in range(8, UNITS):
+            load_x(u)
+        for n in range(1, NB):
+            load_unit(n)
+
+        for r, vec in enumerate([bt, bb, br, bl, bc]):
+            nc.gpsimd.dma_start(
+                out=prw2[2 * r : 2 * r + 2, :], in_=vec.rearrange("(r c) -> r c", c=256)
+            )
+        nc.gpsimd.dma_start(out=prw2[10:20, :], in_=bf1.rearrange("(r c) -> r c", c=256))
+
+        pt1 = psum.tile([P, 512], F32, name="pt1", tag="acc1")
+        nc.tensor.transpose(pt1[:, 0:P], prw1[:].bitcast(F32), ident[:])
+        prm = const.tile([P, 80], F32, name="prm")
+        nc.vector.tensor_copy(out=prm[:], in_=pt1[:, 0:40].bitcast(BF16))
+        ve = const.tile([P, 20], F32, name="ve")
+        nc.vector.tensor_scalar_add(out=ve[:], in0=prm[:, 60:80], scalar1=EPS_BN)
+        sd = const.tile([P, 20], F32, name="sd")
+        nc.scalar.activation(out=sd[:], in_=ve[:], func=ACT.Sqrt)
+        r0 = const.tile([P, 20], F32, name="r0")
+        nc.vector.reciprocal(out=r0[:], in_=sd[:])
+        nw = const.tile([P, 20], F32, name="nw")
+        nc.vector.tensor_mul(out=nw[:], in0=r0[:], in1=r0[:])
+        nc.vector.tensor_mul(out=nw[:], in0=nw[:], in1=ve[:])
+        nc.vector.tensor_scalar(
+            out=nw[:], in0=nw[:], scalar1=-0.5, scalar2=1.5, op0=ALU.mult, op1=ALU.add
+        )
+        bn_s = const.tile([P, 20], F32, name="bn_s")
+        bn_o = const.tile([P, 20], F32, name="bn_o")
+        nc.vector.tensor_mul(out=nw[:], in0=nw[:], in1=r0[:])
+        nc.vector.tensor_mul(out=bn_s[:], in0=nw[:], in1=prm[:, 0:20])
+        nc.vector.tensor_mul(out=nw[:], in0=bn_s[:], in1=prm[:, 40:60])
+        nc.vector.tensor_sub(out=bn_o[:], in0=prm[:, 20:40], in1=nw[:])
+
+        tbs = {}
+        wgrps = {}
+        wcods = {}
+        wscls = {}
+
+        def transposes(n, lo, hi):
+            rawf = raws[n][:].bitcast(F32)
+            for i in range(lo, hi):
+                if i % 4 == 0:
+                    tbs[(n, i // 4)] = psum.tile(
+                        [P, 512], F32, name="tb%d" % (i // 4), tag="tb%d" % (i // 4)
+                    )
+                nc.tensor.transpose(
+                    tbs[(n, i // 4)][:, P * (i % 4) : P * (i % 4) + P],
+                    rawf[:, P * i : P * i + P],
+                    ident[:],
+                )
+
+        def new_codes(n):
+            wgrps[n] = grpp.tile([P, 2 * C], BF16, name="wgrp", tag="wgrp", align_bytes=64)
+            wcods[n] = codp.tile([P, 10 * P], U32, name="wcod", tag="wcod", align_bytes=64)
+            wscls[n] = codp.tile([P, 10 * P], U8, name="wscl", tag="wscl", align_bytes=64)
+
+        def evac(n, k, eng):
+            dst = wgrps[n][:].bitcast(F32)[:, 512 * k : 512 * k + 512].rearrange(
+                "p (n o u) -> p n o u", n=2, u=2
+            )
+            src = tbs[(n, k)][:].rearrange("p (n u o) -> p n o u", n=2, u=2)
+            if eng == "v":
+                nc.vector.tensor_copy(out=dst, in_=src)
+            else:
+                nc.scalar.copy(out=dst, in_=src)
+
+        def quant(n, k0, k1):
+            nc.vector.quantize_mx(
+                out=wcods[n][:, 256 * k0 : 256 * k1].bitcast(FP8X4),
+                scales=wscls[n][:, 256 * k0 : 256 * k1],
+                in_=wgrps[n][:, 1024 * k0 : 1024 * k1],
+            )
+
+        def gelu(g):
+            for col in range(4 * g, 4 * g + 4):
+                nc.scalar.activation(
+                    out=hpl[:, col, :].rearrange("p (b q) -> p b q", b=BATCH),
+                    in_=x_sb[:, col // 2, :, col % 2, :],
+                    func=ACT.Gelu,
+                    bias=bn_o[:, col : col + 1],
+                    scale=bn_s[:, col : col + 1],
+                )
+
+        def regroup(g):
+            src = hpl[:, 4 * g : 4 * g + 4, :].rearrange("p t q -> p q t")
+            if g in POOL_REGROUP:
+                nc.gpsimd.tensor_scalar(
+                    out=hgrp[:, g, :, :], in0=src, scalar1=1.0, scalar2=0.0, op0=ALU.mult, op1=ALU.add
+                )
+            else:
+                nc.vector.tensor_copy(out=hgrp[:, g, :, :], in_=src)
+
+        def quant_act(grp, cod, scl, g):
+            for q0, q1 in ((0, 256), (256, NPIX)):
+                nc.vector.quantize_mx(
+                    out=cod[:, g, q0:q1].bitcast(FP8X4),
+                    scales=scl[:, g, q0:q1],
+                    in_=grp[:, g, q0:q1, :].rearrange("p q t -> p (q t)"),
+                )
+
+        new_codes(0)
+        transposes(0, 0, 10)
+        evac(0, 0, "v")
+        evac(0, 1, "v")
+        quant(0, 0, 2)
+        gelu(0)
+        regroup(0)
+        quant_act(hgrp, hcod, hscl, 0)
+        gelu(1)
+        regroup(1)
+        quant_act(hgrp, hcod, hscl, 1)
+        transposes(0, 10, 20)
+        load_unit(NB)
+        pt2 = psum.tile([P, 512], F32, name="pt2", tag="acc0")
+        nc.tensor.transpose(pt2[:, 0:P], prw2[:].bitcast(F32), ident[:])
+        evac(0, 2, "v")
+        gelu(2)
+        regroup(2)
+        gelu(3)
+        regroup(3)
+        quant_act(hgrp, hcod, hscl, 2)
+        quant_act(hgrp, hcod, hscl, 3)
+        quant(0, 2, 3)
+        gelu(4)
+        regroup(4)
+        quant_act(hgrp, hcod, hscl, 4)
+        bias = const.tile([P, 40], F32, name="bias")
+        nc.vector.tensor_copy(out=bias[:], in_=pt2[:, 0:20].bitcast(BF16))
+        evac(0, 3, "s")
+        evac(0, 4, "s")
+        quant(0, 3, 5)
+
+        accs = {}
+
+        def mx_pass(acc_ap, n, e, g, cod, scl, q0, q1):
+            w0 = P * (G * e + g)
+            nc.tensor.matmul_mx(
+                out=acc_ap,
+                lhsT=wcods[n][:, w0 : w0 + P].bitcast(FP8X4),
+                lhsT_scale=wscls[n][:, w0 : w0 + P],
+                rhs=cod[:, g, q0:q1].bitcast(FP8X4),
+                rhs_scale=scl[:, g, q0:q1],
+                start=(g == 0),
+                stop=(g == G - 1),
+            )
+
+        def stage1(n):
+            pil, u = n // 2, n % 2
+            if u == 0:
+                for j in range(3):
+                    accs[j] = psum.tile([P, 512], F32, name="acc%d" % j, tag="acc%d" % j)
+            for e in range(2):
+                t = 2 * u + e
+                for j in range(3):
+                    for g in range(G):
+                        mx_pass(accs[j][:, P * t : P * t + P], n, e, g, hcod, hscl, P * j, P * j + P)
+            if u == 0:
+                return
+            d = SHIFT[pil]
+            for j in range(3):
+                lo = max(P * j, -d)
+                hi = min(P * j + P, NPIX - d)
+                nc.vector.tensor_tensor(
+                    out=cgrp[:, pil, lo + d : hi + d, :],
+                    in0=accs[j][:].rearrange("p (t q) -> p q t", t=4)[:, lo - P * j : hi - P * j, :],
+                    in1=bias[:, 4 * pil : 4 * pil + 4].unsqueeze(1).to_broadcast([P, hi - lo, 4]),
+                    op=ALU.add,
+                )
+            by_image = cgrp[:, pil, :, :].rearrange("p (b r) t -> p b (r t)", b=BATCH)
+            by_row = cgrp[:, pil, :, :].rearrange("p (n j) t -> p n (j t)", j=12)
+            if d == -12:
+                nc.vector.memset(by_image[:, :, 84 * 4 : 96 * 4], 0.0)
+            elif d == 12:
+                nc.vector.memset(by_image[:, :, 0 : 12 * 4], 0.0)
+            elif d == 1:
+                nc.vector.memset(by_row[:, :, 0:4], 0.0)
+            elif d == -1:
+                nc.vector.memset(by_row[:, :, 44:48], 0.0)
+            quant_act(cgrp, ccod, cscl, pil)
+
+        def stage2(n):
+            uo = n - UNITS
+            osb = outp.tile([P, BATCH, 2, PIX], F32, name="osb", tag="osb")
+            for e in range(2):
+                m = (2 * uo + e) % 3
+                acc = psum.tile([P, 512], F32, name="acc%d" % m, tag="acc%d" % m)
+                for q0, q1 in ((0, 256), (256, NPIX)):
+                    for g in range(G):
+                        mx_pass(acc[:, q0:q1], n, e, g, ccod, cscl, q0, q1)
+                col = 20 + 2 * uo + e
+                nc.scalar.activation(
+                    out=osb[:, :, e, :],
+                    in_=acc[:, 0:NPIX].rearrange("p (b q) -> p b q", b=BATCH),
+                    func=ACT.Identity,
+                    bias=bias[:, col : col + 1],
+                    scale=1.0,
+                )
+            nc.sync.dma_start(
+                out=outv[:, 256 * uo : 256 * uo + 256, :].rearrange("b (p e) q -> p b (e q)", e=2),
+                in_=osb[:].rearrange("p b e q -> p b (e q)"),
+            )
+
+        def multiply(n):
+            if n < UNITS:
+                stage1(n)
+            else:
+                stage2(n)
+
+        for n in range(1, 2 * UNITS):
+            new_codes(n)
+            transposes(n, 0, 20)
+            if n + NB < 2 * UNITS:
+                load_unit(n + NB)
+            on_vector = [1] if n < UNITS else [1, 3]
+            for k in range(5):
+                if k not in on_vector:
+                    evac(n, k, "s")
+            for k in on_vector:
+                evac(n, k, "v")
+            quant(n, 0, 2)
+            quant(n, 2, 4)
+            quant(n, 4, 5)
+            multiply(n - 1)
+        multiply(2 * UNITS - 1)

@@ -21,7 +21,6 @@ UNITS = 10
 NB = 8
 EPS_BN = 1e-5
 SHIFT = [-12, 12, 1, -1, 0]
-POOL_REGROUP = [0, 1, 2]
 
 FLOPS = 2 * 2 * C * C * NPIX
 
@@ -51,16 +50,17 @@ def tile_caterpillarblock_a2_3_np5_pa_kernel(
         hgrp = const.tile([P, G, NPIX, 4], BF16, name="hgrp", align_bytes=64)
         hcod = const.tile([P, G, NPIX], U32, name="hcod", align_bytes=64)
         hscl = const.tile([P, G, NPIX], U8, name="hscl", align_bytes=64)
+        cpl = [const.tile([P, 4, NPIX], BF16, name="cpl%d" % i) for i in range(2)]
         cgrp = const.tile([P, G, NPIX, 4], BF16, name="cgrp", align_bytes=64)
         ccod = const.tile([P, G, NPIX], U32, name="ccod", align_bytes=64)
         cscl = const.tile([P, G, NPIX], U8, name="cscl", align_bytes=64)
 
-        make_identity(nc, ident[:])
         nc.vector.memset(prw1[:], 0.0)
-        nc.vector.memset(prw2[:], 0.0)
+        make_identity(nc, ident[:])
+        nc.gpsimd.memset(prw2[:], 0.0)
 
         for r, vec in enumerate([bn1_g, bn1_b, bn1_m, bn1_v]):
-            nc.scalar.dma_start(
+            nc.sync.dma_start(
                 out=prw1[10 * r : 10 * r + 10, :], in_=vec.rearrange("(r c) -> r c", c=256)
             )
 
@@ -92,12 +92,15 @@ def tile_caterpillarblock_a2_3_np5_pa_kernel(
 
         new_raw(0)
         load_half(0, 0)
-        for u in range(8):
+        for u in range(4):
             load_x(u)
         load_half(0, 1)
-        for u in range(8, UNITS):
+        for u in range(4, UNITS):
             load_x(u)
-        for n in range(1, NB):
+        new_raw(1)
+        load_half(1, 0)
+        load_half(1, 1)
+        for n in range(2, NB):
             load_unit(n)
 
         for r, vec in enumerate([bt, bb, br, bl, bc]):
@@ -105,15 +108,17 @@ def tile_caterpillarblock_a2_3_np5_pa_kernel(
                 out=prw2[2 * r : 2 * r + 2, :], in_=vec.rearrange("(r c) -> r c", c=256)
             )
         nc.gpsimd.dma_start(out=prw2[10:20, :], in_=bf1.rearrange("(r c) -> r c", c=256))
+        nc.gpsimd.memset(cpl[0][:], 0.0)
+        nc.gpsimd.memset(cpl[1][:], 0.0)
 
         pt1 = psum.tile([P, 512], F32, name="pt1", tag="acc1")
         nc.tensor.transpose(pt1[:, 0:P], prw1[:].bitcast(F32), ident[:])
-        prm = const.tile([P, 80], F32, name="prm")
-        nc.vector.tensor_copy(out=prm[:], in_=pt1[:, 0:40].bitcast(BF16))
         ve = const.tile([P, 20], F32, name="ve")
-        nc.vector.tensor_scalar_add(out=ve[:], in0=prm[:, 60:80], scalar1=EPS_BN)
+        nc.vector.tensor_scalar_add(out=ve[:], in0=pt1[:, 30:40].bitcast(BF16), scalar1=EPS_BN)
         sd = const.tile([P, 20], F32, name="sd")
         nc.scalar.activation(out=sd[:], in_=ve[:], func=ACT.Sqrt)
+        prm = const.tile([P, 60], F32, name="prm")
+        nc.vector.tensor_copy(out=prm[:], in_=pt1[:, 0:30].bitcast(BF16))
         r0 = const.tile([P, 20], F32, name="r0")
         nc.vector.reciprocal(out=r0[:], in_=sd[:])
         nw = const.tile([P, 20], F32, name="nw")
@@ -169,66 +174,65 @@ def tile_caterpillarblock_a2_3_np5_pa_kernel(
                 in_=wgrps[n][:, 1024 * k0 : 1024 * k1],
             )
 
-        def gelu(g):
+        def gelu(g, b0, b1):
             for col in range(4 * g, 4 * g + 4):
                 nc.scalar.activation(
-                    out=hpl[:, col, :].rearrange("p (b q) -> p b q", b=BATCH),
-                    in_=x_sb[:, col // 2, :, col % 2, :],
+                    out=hpl[:, col, PIX * b0 : PIX * b1].rearrange("p (b q) -> p b q", q=PIX),
+                    in_=x_sb[:, col // 2, b0:b1, col % 2, :],
                     func=ACT.Gelu,
                     bias=bn_o[:, col : col + 1],
                     scale=bn_s[:, col : col + 1],
                 )
 
-        def regroup(g):
-            src = hpl[:, 4 * g : 4 * g + 4, :].rearrange("p t q -> p q t")
-            if g in POOL_REGROUP:
-                nc.gpsimd.tensor_scalar(
-                    out=hgrp[:, g, :, :], in0=src, scalar1=1.0, scalar2=0.0, op0=ALU.mult, op1=ALU.add
-                )
-            else:
-                nc.vector.tensor_copy(out=hgrp[:, g, :, :], in_=src)
+        def regroup(planes, grp, g, q0, q1):
+            nc.vector.tensor_copy(
+                out=grp[:, g, q0:q1, :].rearrange("p (c i) t -> p c t i", i=4),
+                in_=planes[:, :, q0:q1].rearrange("p t (c i) -> p c t i", i=4),
+            )
+
+        def quant_part(grp, cod, scl, g, q0, q1):
+            nc.vector.quantize_mx(
+                out=cod[:, g, q0:q1].bitcast(FP8X4),
+                scales=scl[:, g, q0:q1],
+                in_=grp[:, g, q0:q1, :].rearrange("p q t -> p (q t)"),
+            )
 
         def quant_act(grp, cod, scl, g):
-            for q0, q1 in ((0, 256), (256, NPIX)):
-                nc.vector.quantize_mx(
-                    out=cod[:, g, q0:q1].bitcast(FP8X4),
-                    scales=scl[:, g, q0:q1],
-                    in_=grp[:, g, q0:q1, :].rearrange("p q t -> p (q t)"),
-                )
+            quant_part(grp, cod, scl, g, 0, 256)
+            quant_part(grp, cod, scl, g, 256, NPIX)
+
+        def h_chunk(g):
+            gelu(g, 0, BATCH)
+            regroup(hpl[:, 4 * g : 4 * g + 4, :], hgrp, g, 0, NPIX)
+            quant_act(hgrp, hcod, hscl, g)
 
         new_codes(0)
         transposes(0, 0, 10)
         evac(0, 0, "v")
         evac(0, 1, "v")
         quant(0, 0, 2)
-        gelu(0)
-        regroup(0)
-        quant_act(hgrp, hcod, hscl, 0)
-        gelu(1)
-        regroup(1)
-        quant_act(hgrp, hcod, hscl, 1)
+        h_chunk(0)
+        h_chunk(1)
         transposes(0, 10, 20)
         load_unit(NB)
-        pt2 = psum.tile([P, 512], F32, name="pt2", tag="acc0")
+        pt2 = psum.tile([P, 512], F32, name="pt2", tag="acc2")
         nc.tensor.transpose(pt2[:, 0:P], prw2[:].bitcast(F32), ident[:])
         evac(0, 2, "v")
-        gelu(2)
-        regroup(2)
-        gelu(3)
-        regroup(3)
-        quant_act(hgrp, hcod, hscl, 2)
-        quant_act(hgrp, hcod, hscl, 3)
+        h_chunk(2)
         quant(0, 2, 3)
-        gelu(4)
-        regroup(4)
-        quant_act(hgrp, hcod, hscl, 4)
+        h_chunk(3)
+        last = hpl[:, 16:20, :]
+        gelu(4, 0, 3)
+        regroup(last, hgrp, 4, 0, 256)
+        quant_part(hgrp, hcod, hscl, 4, 0, 256)
+        gelu(4, 3, 4)
+        regroup(last, hgrp, 4, 256, NPIX)
+        quant_part(hgrp, hcod, hscl, 4, 256, NPIX)
         bias = const.tile([P, 40], F32, name="bias")
         nc.vector.tensor_copy(out=bias[:], in_=pt2[:, 0:20].bitcast(BF16))
         evac(0, 3, "s")
         evac(0, 4, "s")
         quant(0, 3, 5)
-
-        accs = {}
 
         def mx_pass(acc_ap, n, e, g, cod, scl, q0, q1):
             w0 = P * (G * e + g)
@@ -242,28 +246,33 @@ def tile_caterpillarblock_a2_3_np5_pa_kernel(
                 stop=(g == G - 1),
             )
 
+        def products(n, e, cod, scl):
+            m = (2 * n + e) % 3
+            acc = psum.tile([P, 512], F32, name="acc%d" % m, tag="acc%d" % m)
+            for q0, q1 in ((0, 256), (256, NPIX)):
+                for g in range(G):
+                    mx_pass(acc[:, q0:q1], n, e, g, cod, scl, q0, q1)
+            return acc
+
         def stage1(n):
             pil, u = n // 2, n % 2
-            if u == 0:
-                for j in range(3):
-                    accs[j] = psum.tile([P, 512], F32, name="acc%d" % j, tag="acc%d" % j)
+            d = SHIFT[pil]
+            lo = max(0, -d)
+            hi = min(NPIX, NPIX - d)
+            planes = cpl[pil % 2]
             for e in range(2):
                 t = 2 * u + e
-                for j in range(3):
-                    for g in range(G):
-                        mx_pass(accs[j][:, P * t : P * t + P], n, e, g, hcod, hscl, P * j, P * j + P)
+                acc = products(n, e, hcod, hscl)
+                nc.scalar.activation(
+                    out=planes[:, t, lo + d : hi + d],
+                    in_=acc[:, lo:hi],
+                    func=ACT.Identity,
+                    bias=bias[:, 4 * pil + t : 4 * pil + t + 1],
+                    scale=1.0,
+                )
             if u == 0:
                 return
-            d = SHIFT[pil]
-            for j in range(3):
-                lo = max(P * j, -d)
-                hi = min(P * j + P, NPIX - d)
-                nc.vector.tensor_tensor(
-                    out=cgrp[:, pil, lo + d : hi + d, :],
-                    in0=accs[j][:].rearrange("p (t q) -> p q t", t=4)[:, lo - P * j : hi - P * j, :],
-                    in1=bias[:, 4 * pil : 4 * pil + 4].unsqueeze(1).to_broadcast([P, hi - lo, 4]),
-                    op=ALU.add,
-                )
+            regroup(planes, cgrp, pil, 0, NPIX)
             by_image = cgrp[:, pil, :, :].rearrange("p (b r) t -> p b (r t)", b=BATCH)
             by_row = cgrp[:, pil, :, :].rearrange("p (n j) t -> p n (j t)", j=12)
             if d == -12:
@@ -280,11 +289,7 @@ def tile_caterpillarblock_a2_3_np5_pa_kernel(
             uo = n - UNITS
             osb = outp.tile([P, BATCH, 2, PIX], F32, name="osb", tag="osb")
             for e in range(2):
-                m = (2 * uo + e) % 3
-                acc = psum.tile([P, 512], F32, name="acc%d" % m, tag="acc%d" % m)
-                for q0, q1 in ((0, 256), (256, NPIX)):
-                    for g in range(G):
-                        mx_pass(acc[:, q0:q1], n, e, g, ccod, cscl, q0, q1)
+                acc = products(n, e, ccod, cscl)
                 col = 20 + 2 * uo + e
                 nc.scalar.activation(
                     out=osb[:, :, e, :],

@@ -18,7 +18,7 @@ PIX = 96
 NPIX = BATCH * PIX
 G = 5
 UNITS = 10
-NB = 8
+NB = 7
 EPS_BN = 1e-5
 SHIFT = [-12, 12, 1, -1, 0]
 
@@ -36,8 +36,8 @@ def tile_caterpillarblock_a2_3_np5_pa_kernel(
     with ExitStack() as ctx:
         const = ctx.enter_context(tc.tile_pool(name="const", bufs=1))
         rawp = ctx.enter_context(tc.tile_pool(name="rawp", bufs=NB))
-        grpp = ctx.enter_context(tc.tile_pool(name="grpp", bufs=2))
-        codp = ctx.enter_context(tc.tile_pool(name="codp", bufs=3))
+        grpp = ctx.enter_context(tc.tile_pool(name="grpp", bufs=3))
+        codp = ctx.enter_context(tc.tile_pool(name="codp", bufs=4))
         outp = ctx.enter_context(tc.tile_pool(name="outp", bufs=3))
         psum = ctx.enter_context(tc.psum_pool(name="psum", bufs=1))
         ctx.enter_context(tc.manual_schedule())
@@ -309,19 +309,39 @@ def tile_caterpillarblock_a2_3_np5_pa_kernel(
             else:
                 stage2(n)
 
-        for n in range(1, 2 * UNITS):
+        def prepare(n):
             new_codes(n)
             transposes(n, 0, 20)
             if n + NB < 2 * UNITS:
                 load_unit(n + NB)
-            on_vector = [1] if n < UNITS else [1, 3]
-            for k in range(5):
-                if k not in on_vector:
-                    evac(n, k, "s")
-            for k in on_vector:
-                evac(n, k, "v")
-            quant(n, 0, 2)
-            quant(n, 2, 4)
-            quant(n, 4, 5)
-            multiply(n - 1)
+
+        def run_of_transposes(a, b):
+            prepare(a)
+            evac(a, 0, "s")
+            evac(a, 1, "v")
+            quant(a, 0, 2)
+            evac(a, 2, "s")
+            evac(a, 3, "s")
+            evac(a, 4, "v")
+            quant(a, 2, 4)
+            if b is None:
+                quant(a, 4, 5)
+                return
+            prepare(b)
+            evac(b, 0, "s")
+            evac(b, 1, "v")
+            quant(a, 4, 5)
+            evac(b, 2, "s")
+            evac(b, 3, "s")
+            evac(b, 4, "v")
+            quant(b, 0, 2)
+            quant(b, 2, 4)
+            quant(b, 4, 5)
+
+        run_of_transposes(1, None)
+        multiply(0)
+        for a in range(2, 2 * UNITS, 2):
+            run_of_transposes(a, a + 1)
+            multiply(a - 1)
+            multiply(a)
         multiply(2 * UNITS - 1)

@@ -18,7 +18,7 @@ PIX = 96
 NPIX = BATCH * PIX
 G = 5
 UNITS = 10
-NB = 7
+NB = 8
 EPS_BN = 1e-5
 SHIFT = [-12, 12, 1, -1, 0]
 
@@ -36,8 +36,8 @@ def tile_caterpillarblock_a2_3_np5_pa_kernel(
     with ExitStack() as ctx:
         const = ctx.enter_context(tc.tile_pool(name="const", bufs=1))
         rawp = ctx.enter_context(tc.tile_pool(name="rawp", bufs=NB))
-        grpp = ctx.enter_context(tc.tile_pool(name="grpp", bufs=3))
-        codp = ctx.enter_context(tc.tile_pool(name="codp", bufs=4))
+        grpp = ctx.enter_context(tc.tile_pool(name="grpp", bufs=2))
+        codp = ctx.enter_context(tc.tile_pool(name="codp", bufs=3))
         outp = ctx.enter_context(tc.tile_pool(name="outp", bufs=3))
         psum = ctx.enter_context(tc.psum_pool(name="psum", bufs=1))
         ctx.enter_context(tc.manual_schedule())
@@ -309,39 +309,19 @@ def tile_caterpillarblock_a2_3_np5_pa_kernel(
             else:
                 stage2(n)
 
-        def prepare(n):
+        for n in range(1, 2 * UNITS):
             new_codes(n)
             transposes(n, 0, 20)
             if n + NB < 2 * UNITS:
                 load_unit(n + NB)
-
-        def run_of_transposes(a, b):
-            prepare(a)
-            evac(a, 0, "s")
-            evac(a, 1, "v")
-            quant(a, 0, 2)
-            evac(a, 2, "s")
-            evac(a, 3, "s")
-            evac(a, 4, "v")
-            quant(a, 2, 4)
-            if b is None:
-                quant(a, 4, 5)
-                return
-            prepare(b)
-            evac(b, 0, "s")
-            evac(b, 1, "v")
-            quant(a, 4, 5)
-            evac(b, 2, "s")
-            evac(b, 3, "s")
-            evac(b, 4, "v")
-            quant(b, 0, 2)
-            quant(b, 2, 4)
-            quant(b, 4, 5)
-
-        run_of_transposes(1, None)
-        multiply(0)
-        for a in range(2, 2 * UNITS, 2):
-            run_of_transposes(a, a + 1)
-            multiply(a - 1)
-            multiply(a)
+            on_vector = [1, 3]
+            for k in range(5):
+                if k not in on_vector:
+                    evac(n, k, "s")
+            for k in on_vector:
+                evac(n, k, "v")
+            quant(n, 0, 2)
+            quant(n, 2, 4)
+            quant(n, 4, 5)
+            multiply(n - 1)
         multiply(2 * UNITS - 1)

@@ -298,10 +298,18 @@ def tile_caterpillarblock_a2_3_np5_pa_kernel(
                     bias=bias[:, col : col + 1],
                     scale=1.0,
                 )
-            nc.sync.dma_start(
-                out=outv[:, 256 * uo : 256 * uo + 256, :].rearrange("b (p e) q -> p b (e q)", e=2),
-                in_=osb[:].rearrange("p b e q -> p b (e q)"),
-            )
+                if n == 2 * UNITS - 1:
+                    nc.sync.dma_start(
+                        out=outv[:, 256 * uo : 256 * uo + 256, :].rearrange(
+                            "b (p e) q -> p e b q", e=2
+                        )[:, e, :, :],
+                        in_=osb[:, :, e, :],
+                    )
+            if n < 2 * UNITS - 1:
+                nc.sync.dma_start(
+                    out=outv[:, 256 * uo : 256 * uo + 256, :].rearrange("b (p e) q -> p b (e q)", e=2),
+                    in_=osb[:].rearrange("p b e q -> p b (e q)"),
+                )
 
         def multiply(n):
             if n < UNITS:
@@ -314,14 +322,23 @@ def tile_caterpillarblock_a2_3_np5_pa_kernel(
             transposes(n, 0, 20)
             if n + NB < 2 * UNITS:
                 load_unit(n + NB)
-            on_vector = [1, 3]
-            for k in range(5):
-                if k not in on_vector:
-                    evac(n, k, "s")
-            for k in on_vector:
-                evac(n, k, "v")
-            quant(n, 0, 2)
-            quant(n, 2, 4)
-            quant(n, 4, 5)
+            if n < 2 * UNITS - 1:
+                evac(n, 2, "s")
+                evac(n, 4, "s")
+                evac(n, 0, "s")
+                evac(n, 3, "v")
+                evac(n, 1, "v")
+                quant(n, 2, 4)
+                quant(n, 4, 5)
+                quant(n, 0, 2)
+            else:
+                evac(n, 0, "s")
+                evac(n, 2, "s")
+                evac(n, 4, "s")
+                evac(n, 1, "v")
+                evac(n, 3, "v")
+                quant(n, 0, 2)
+                quant(n, 2, 4)
+                quant(n, 4, 5)
             multiply(n - 1)
         multiply(2 * UNITS - 1)

@@ -201,8 +201,23 @@ def tile_caterpillarblock_a2_3_np5_pa_kernel(
             quant_part(grp, cod, scl, g, 0, 256)
             quant_part(grp, cod, scl, g, 256, NPIX)
 
+        warm = psum.tile([P, 512], F32, name="warm", tag="acc0")
+
+        def keep_clock(g):
+            for col in range(4 * g, 4 * g + 4):
+                for i in range(2):
+                    nc.tensor.matmul(
+                        out=warm[:, 0:256],
+                        lhsT=prw1[:, 0:P],
+                        rhs=hpl[:, col, 0:256],
+                        start=True,
+                        stop=True,
+                    )
+
         def h_chunk(g):
             gelu(g, 0, BATCH)
+            if g >= 2:
+                keep_clock(g)
             regroup(hpl[:, 4 * g : 4 * g + 4, :], hgrp, g, 0, NPIX)
             quant_act(hgrp, hcod, hscl, g)
 
@@ -223,6 +238,7 @@ def tile_caterpillarblock_a2_3_np5_pa_kernel(
         h_chunk(3)
         last = hpl[:, 16:20, :]
         gelu(4, 0, 3)
+        keep_clock(4)
         regroup(last, hgrp, 4, 0, 256)
         quant_part(hgrp, hcod, hscl, 4, 0, 256)
         gelu(4, 3, 4)
@@ -317,7 +333,21 @@ def tile_caterpillarblock_a2_3_np5_pa_kernel(
             else:
                 stage2(n)
 
-        for n in range(1, 2 * UNITS):
+        new_codes(1)
+        transposes(1, 0, 10)
+        evac(1, 0, "s")
+        evac(1, 1, "v")
+        quant(1, 0, 2)
+        multiply(0)
+        transposes(1, 10, 20)
+        load_unit(1 + NB)
+        evac(1, 2, "s")
+        evac(1, 3, "v")
+        evac(1, 4, "s")
+        quant(1, 2, 4)
+        quant(1, 4, 5)
+
+        for n in range(2, 2 * UNITS):
             new_codes(n)
             transposes(n, 0, 20)
             if n + NB < 2 * UNITS:

@@ -201,23 +201,8 @@ def tile_caterpillarblock_a2_3_np5_pa_kernel(
             quant_part(grp, cod, scl, g, 0, 256)
             quant_part(grp, cod, scl, g, 256, NPIX)
 
-        warm = psum.tile([P, 512], F32, name="warm", tag="acc0")
-
-        def keep_clock(g):
-            for col in range(4 * g, 4 * g + 4):
-                for i in range(2):
-                    nc.tensor.matmul(
-                        out=warm[:, 0:256],
-                        lhsT=prw1[:, 0:P],
-                        rhs=hpl[:, col, 0:256],
-                        start=True,
-                        stop=True,
-                    )
-
         def h_chunk(g):
             gelu(g, 0, BATCH)
-            if g >= 2:
-                keep_clock(g)
             regroup(hpl[:, 4 * g : 4 * g + 4, :], hgrp, g, 0, NPIX)
             quant_act(hgrp, hcod, hscl, g)
 
@@ -238,7 +223,6 @@ def tile_caterpillarblock_a2_3_np5_pa_kernel(
         h_chunk(3)
         last = hpl[:, 16:20, :]
         gelu(4, 0, 3)
-        keep_clock(4)
         regroup(last, hgrp, 4, 0, 256)
         quant_part(hgrp, hcod, hscl, 4, 0, 256)
         gelu(4, 3, 4)
@@ -270,25 +254,56 @@ def tile_caterpillarblock_a2_3_np5_pa_kernel(
                     mx_pass(acc[:, q0:q1], n, e, g, cod, scl, q0, q1)
             return acc
 
-        def stage1(n):
-            pil, u = n // 2, n % 2
-            d = SHIFT[pil]
-            lo = max(0, -d)
-            hi = min(NPIX, NPIX - d)
-            planes = cpl[pil % 2]
-            for e in range(2):
+        osbs = {}
+
+        def tile_products(n, e):
+            if n < UNITS:
+                pil, u = n // 2, n % 2
+                d = SHIFT[pil]
+                lo = max(0, -d)
+                hi = min(NPIX, NPIX - d)
                 t = 2 * u + e
                 acc = products(n, e, hcod, hscl)
                 nc.scalar.activation(
-                    out=planes[:, t, lo + d : hi + d],
+                    out=cpl[pil % 2][:, t, lo + d : hi + d],
                     in_=acc[:, lo:hi],
                     func=ACT.Identity,
                     bias=bias[:, 4 * pil + t : 4 * pil + t + 1],
                     scale=1.0,
                 )
-            if u == 0:
                 return
-            regroup(planes, cgrp, pil, 0, NPIX)
+            uo = n - UNITS
+            if e == 0:
+                osbs[n] = outp.tile([P, BATCH, 2, PIX], F32, name="osb", tag="osb")
+            osb = osbs[n]
+            acc = products(n, e, ccod, cscl)
+            col = 20 + 2 * uo + e
+            nc.scalar.activation(
+                out=osb[:, :, e, :],
+                in_=acc[:, 0:NPIX].rearrange("p (b q) -> p b q", b=BATCH),
+                func=ACT.Identity,
+                bias=bias[:, col : col + 1],
+                scale=1.0,
+            )
+            if n == 2 * UNITS - 1:
+                nc.sync.dma_start(
+                    out=outv[:, 256 * uo : 256 * uo + 256, :].rearrange("b (p e) q -> p e b q", e=2)[
+                        :, e, :, :
+                    ],
+                    in_=osb[:, :, e, :],
+                )
+            elif e == 1:
+                nc.sync.dma_start(
+                    out=outv[:, 256 * uo : 256 * uo + 256, :].rearrange("b (p e) q -> p b (e q)", e=2),
+                    in_=osb[:].rearrange("p b e q -> p b (e q)"),
+                )
+
+        def finish_pillar(n):
+            if n >= UNITS or n % 2 == 0:
+                return
+            pil = n // 2
+            d = SHIFT[pil]
+            regroup(cpl[pil % 2], cgrp, pil, 0, NPIX)
             by_image = cgrp[:, pil, :, :].rearrange("p (b r) t -> p b (r t)", b=BATCH)
             by_row = cgrp[:, pil, :, :].rearrange("p (n j) t -> p n (j t)", j=12)
             if d == -12:
@@ -301,74 +316,23 @@ def tile_caterpillarblock_a2_3_np5_pa_kernel(
                 nc.vector.memset(by_row[:, :, 44:48], 0.0)
             quant_act(cgrp, ccod, cscl, pil)
 
-        def stage2(n):
-            uo = n - UNITS
-            osb = outp.tile([P, BATCH, 2, PIX], F32, name="osb", tag="osb")
-            for e in range(2):
-                acc = products(n, e, ccod, cscl)
-                col = 20 + 2 * uo + e
-                nc.scalar.activation(
-                    out=osb[:, :, e, :],
-                    in_=acc[:, 0:NPIX].rearrange("p (b q) -> p b q", b=BATCH),
-                    func=ACT.Identity,
-                    bias=bias[:, col : col + 1],
-                    scale=1.0,
-                )
-                if n == 2 * UNITS - 1:
-                    nc.sync.dma_start(
-                        out=outv[:, 256 * uo : 256 * uo + 256, :].rearrange(
-                            "b (p e) q -> p e b q", e=2
-                        )[:, e, :, :],
-                        in_=osb[:, :, e, :],
-                    )
-            if n < 2 * UNITS - 1:
-                nc.sync.dma_start(
-                    out=outv[:, 256 * uo : 256 * uo + 256, :].rearrange("b (p e) q -> p b (e q)", e=2),
-                    in_=osb[:].rearrange("p b e q -> p b (e q)"),
-                )
-
-        def multiply(n):
-            if n < UNITS:
-                stage1(n)
-            else:
-                stage2(n)
-
-        new_codes(1)
-        transposes(1, 0, 10)
-        evac(1, 0, "s")
-        evac(1, 1, "v")
-        quant(1, 0, 2)
-        multiply(0)
-        transposes(1, 10, 20)
-        load_unit(1 + NB)
-        evac(1, 2, "s")
-        evac(1, 3, "v")
-        evac(1, 4, "s")
-        quant(1, 2, 4)
-        quant(1, 4, 5)
-
-        for n in range(2, 2 * UNITS):
+        for n in range(1, 2 * UNITS):
             new_codes(n)
-            transposes(n, 0, 20)
+            transposes(n, 0, 12)
+            evac(n, 0, "s")
+            evac(n, 1, "v")
+            evac(n, 2, "s")
+            quant(n, 0, 2)
+            quant(n, 2, 3)
+            if n == 1:
+                tile_products(0, 0)
+            tile_products(n - 1, 1)
+            transposes(n, 12, 20)
             if n + NB < 2 * UNITS:
                 load_unit(n + NB)
-            if n < 2 * UNITS - 1:
-                evac(n, 2, "s")
-                evac(n, 4, "s")
-                evac(n, 0, "s")
-                evac(n, 3, "v")
-                evac(n, 1, "v")
-                quant(n, 2, 4)
-                quant(n, 4, 5)
-                quant(n, 0, 2)
-            else:
-                evac(n, 0, "s")
-                evac(n, 2, "s")
-                evac(n, 4, "s")
-                evac(n, 1, "v")
-                evac(n, 3, "v")
-                quant(n, 0, 2)
-                quant(n, 2, 4)
-                quant(n, 4, 5)
-            multiply(n - 1)
-        multiply(2 * UNITS - 1)
+            evac(n, 3, "v")
+            evac(n, 4, "s")
+            quant(n, 3, 5)
+            finish_pillar(n - 1)
+            tile_products(n, 0)
+        tile_products(2 * UNITS - 1, 1)

@@ -18,7 +18,7 @@ PIX = 96
 NPIX = BATCH * PIX
 G = 5
 UNITS = 10
-NB = 8
+NB = 7
 EPS_BN = 1e-5
 SHIFT = [-12, 12, 1, -1, 0]
 
@@ -36,8 +36,8 @@ def tile_caterpillarblock_a2_3_np5_pa_kernel(
     with ExitStack() as ctx:
         const = ctx.enter_context(tc.tile_pool(name="const", bufs=1))
         rawp = ctx.enter_context(tc.tile_pool(name="rawp", bufs=NB))
-        grpp = ctx.enter_context(tc.tile_pool(name="grpp", bufs=2))
-        codp = ctx.enter_context(tc.tile_pool(name="codp", bufs=3))
+        grpp = ctx.enter_context(tc.tile_pool(name="grpp", bufs=3))
+        codp = ctx.enter_context(tc.tile_pool(name="codp", bufs=4))
         outp = ctx.enter_context(tc.tile_pool(name="outp", bufs=3))
         psum = ctx.enter_context(tc.psum_pool(name="psum", bufs=1))
         ctx.enter_context(tc.manual_schedule())
@@ -316,23 +316,54 @@ def tile_caterpillarblock_a2_3_np5_pa_kernel(
                 nc.vector.memset(by_row[:, :, 44:48], 0.0)
             quant_act(cgrp, ccod, cscl, pil)
 
-        for n in range(1, 2 * UNITS):
+        def multiply(n):
+            tile_products(n, 0)
+            tile_products(n, 1)
+
+        def prepare(n):
             new_codes(n)
-            transposes(n, 0, 12)
-            evac(n, 0, "s")
-            evac(n, 1, "v")
-            evac(n, 2, "s")
-            quant(n, 0, 2)
-            quant(n, 2, 3)
-            if n == 1:
-                tile_products(0, 0)
-            tile_products(n - 1, 1)
-            transposes(n, 12, 20)
+            transposes(n, 0, 20)
             if n + NB < 2 * UNITS:
                 load_unit(n + NB)
-            evac(n, 3, "v")
-            evac(n, 4, "s")
-            quant(n, 3, 5)
-            finish_pillar(n - 1)
-            tile_products(n, 0)
-        tile_products(2 * UNITS - 1, 1)
+
+        def run_of_two(a, pending):
+            b = a + 1
+            prepare(a)
+            evac(a, 0, "s")
+            evac(a, 1, "v")
+            evac(a, 2, "s")
+            evac(a, 3, "v")
+            evac(a, 4, "s")
+            prepare(b)
+            if pending is not None:
+                finish_pillar(pending)
+            quant(a, 0, 2)
+            evac(b, 0, "s")
+            evac(b, 1, "s")
+            evac(b, 2, "v")
+            evac(b, 3, "s")
+            evac(b, 4, "s")
+            quant(a, 2, 4)
+            quant(a, 4, 5)
+            quant(b, 0, 2)
+            quant(b, 2, 4)
+            quant(b, 4, 5)
+
+        prepare(1)
+        evac(1, 0, "s")
+        evac(1, 1, "v")
+        evac(1, 2, "s")
+        evac(1, 3, "v")
+        evac(1, 4, "s")
+        quant(1, 0, 2)
+        quant(1, 2, 4)
+        quant(1, 4, 5)
+        multiply(0)
+        run_of_two(2, None)
+        multiply(1)
+        for a in range(4, 2 * UNITS, 2):
+            run_of_two(a, a - 3)
+            multiply(a - 2)
+            multiply(a - 1)
+        multiply(2 * UNITS - 2)
+        multiply(2 * UNITS - 1)

@@ -60,7 +60,7 @@ def tile_caterpillarblock_a2_3_np5_pa_kernel(
         nc.gpsimd.memset(prw2[:], 0.0)
 
         for r, vec in enumerate([bn1_g, bn1_b, bn1_m, bn1_v]):
-            nc.sync.dma_start(
+            nc.scalar.dma_start(
                 out=prw1[10 * r : 10 * r + 10, :], in_=vec.rearrange("(r c) -> r c", c=256)
             )
 
@@ -90,17 +90,18 @@ def tile_caterpillarblock_a2_3_np5_pa_kernel(
                 in_=xv[:, 256 * u : 256 * u + 256, :].rearrange("b (p e) q -> p b (e q)", e=2),
             )
 
-        new_raw(0)
-        load_half(0, 0)
-        for u in range(4):
+        def load_halves(n):
+            new_raw(n)
+            load_half(n, 0)
+            load_half(n, 1)
+
+        load_halves(0)
+        for u in range(UNITS):
             load_x(u)
-        load_half(0, 1)
-        for u in range(4, UNITS):
-            load_x(u)
-        new_raw(1)
-        load_half(1, 0)
-        load_half(1, 1)
-        for n in range(2, NB):
+        load_halves(1)
+        load_halves(2)
+        load_halves(3)
+        for n in range(4, NB):
             load_unit(n)
 
         for r, vec in enumerate([bt, bb, br, bl, bc]):
@@ -119,20 +120,26 @@ def tile_caterpillarblock_a2_3_np5_pa_kernel(
         nc.scalar.activation(out=sd[:], in_=ve[:], func=ACT.Sqrt)
         prm = const.tile([P, 60], F32, name="prm")
         nc.vector.tensor_copy(out=prm[:], in_=pt1[:, 0:30].bitcast(BF16))
+        warm = const.tile([P, 1], F32, name="warm")
+        nc.scalar.activation(out=warm[:], in_=sd[:, 0:1], func=ACT.Gelu)
         r0 = const.tile([P, 20], F32, name="r0")
         nc.vector.reciprocal(out=r0[:], in_=sd[:])
-        nw = const.tile([P, 20], F32, name="nw")
-        nc.vector.tensor_mul(out=nw[:], in0=r0[:], in1=r0[:])
-        nc.vector.tensor_mul(out=nw[:], in0=nw[:], in1=ve[:])
-        nc.vector.tensor_scalar(
-            out=nw[:], in0=nw[:], scalar1=-0.5, scalar2=1.5, op0=ALU.mult, op1=ALU.add
+        na = const.tile([P, 20], F32, name="na")
+        nb = const.tile([P, 20], F32, name="nb")
+        rg = const.tile([P, 20], F32, name="rg")
+        nc.vector.scalar_tensor_tensor(
+            out=na[:], in0=r0[:], scalar=-0.5, in1=ve[:], op0=ALU.mult, op1=ALU.mult
         )
+        nc.vector.tensor_mul(out=rg[:], in0=r0[:], in1=prm[:, 0:20])
+        nc.vector.tensor_mul(out=nb[:], in0=na[:], in1=r0[:])
         bn_s = const.tile([P, 20], F32, name="bn_s")
         bn_o = const.tile([P, 20], F32, name="bn_o")
-        nc.vector.tensor_mul(out=nw[:], in0=nw[:], in1=r0[:])
-        nc.vector.tensor_mul(out=bn_s[:], in0=nw[:], in1=prm[:, 0:20])
-        nc.vector.tensor_mul(out=nw[:], in0=bn_s[:], in1=prm[:, 40:60])
-        nc.vector.tensor_sub(out=bn_o[:], in0=prm[:, 20:40], in1=nw[:])
+        ms = const.tile([P, 20], F32, name="ms")
+        nc.vector.scalar_tensor_tensor(
+            out=bn_s[:], in0=nb[:], scalar=1.5, in1=rg[:], op0=ALU.add, op1=ALU.mult
+        )
+        nc.vector.tensor_mul(out=ms[:], in0=bn_s[:], in1=prm[:, 40:60])
+        nc.vector.tensor_sub(out=bn_o[:], in0=prm[:, 20:40], in1=ms[:])
 
         tbs = {}
         wgrps = {}
@@ -201,39 +208,6 @@ def tile_caterpillarblock_a2_3_np5_pa_kernel(
             quant_part(grp, cod, scl, g, 0, 256)
             quant_part(grp, cod, scl, g, 256, NPIX)
 
-        def h_chunk(g):
-            gelu(g, 0, BATCH)
-            regroup(hpl[:, 4 * g : 4 * g + 4, :], hgrp, g, 0, NPIX)
-            quant_act(hgrp, hcod, hscl, g)
-
-        new_codes(0)
-        transposes(0, 0, 10)
-        evac(0, 0, "v")
-        evac(0, 1, "v")
-        quant(0, 0, 2)
-        h_chunk(0)
-        h_chunk(1)
-        transposes(0, 10, 20)
-        load_unit(NB)
-        pt2 = psum.tile([P, 512], F32, name="pt2", tag="acc2")
-        nc.tensor.transpose(pt2[:, 0:P], prw2[:].bitcast(F32), ident[:])
-        evac(0, 2, "v")
-        h_chunk(2)
-        quant(0, 2, 3)
-        h_chunk(3)
-        last = hpl[:, 16:20, :]
-        gelu(4, 0, 3)
-        regroup(last, hgrp, 4, 0, 256)
-        quant_part(hgrp, hcod, hscl, 4, 0, 256)
-        gelu(4, 3, 4)
-        regroup(last, hgrp, 4, 256, NPIX)
-        quant_part(hgrp, hcod, hscl, 4, 256, NPIX)
-        bias = const.tile([P, 40], F32, name="bias")
-        nc.vector.tensor_copy(out=bias[:], in_=pt2[:, 0:20].bitcast(BF16))
-        evac(0, 3, "s")
-        evac(0, 4, "s")
-        quant(0, 3, 5)
-
         def mx_pass(acc_ap, n, e, g, cod, scl, q0, q1):
             w0 = P * (G * e + g)
             nc.tensor.matmul_mx(
@@ -257,13 +231,15 @@ def tile_caterpillarblock_a2_3_np5_pa_kernel(
         osbs = {}
 
         def tile_products(n, e):
+            tile_out(n, e, products(n, e, hcod, hscl) if n < UNITS else products(n, e, ccod, cscl))
+
+        def tile_out(n, e, acc):
             if n < UNITS:
                 pil, u = n // 2, n % 2
                 d = SHIFT[pil]
                 lo = max(0, -d)
                 hi = min(NPIX, NPIX - d)
                 t = 2 * u + e
-                acc = products(n, e, hcod, hscl)
                 nc.scalar.activation(
                     out=cpl[pil % 2][:, t, lo + d : hi + d],
                     in_=acc[:, lo:hi],
@@ -276,7 +252,6 @@ def tile_caterpillarblock_a2_3_np5_pa_kernel(
             if e == 0:
                 osbs[n] = outp.tile([P, BATCH, 2, PIX], F32, name="osb", tag="osb")
             osb = osbs[n]
-            acc = products(n, e, ccod, cscl)
             col = 20 + 2 * uo + e
             nc.scalar.activation(
                 out=osb[:, :, e, :],
@@ -349,21 +324,74 @@ def tile_caterpillarblock_a2_3_np5_pa_kernel(
             quant(b, 2, 4)
             quant(b, 4, 5)
 
-        prepare(1)
-        evac(1, 0, "s")
-        evac(1, 1, "v")
-        evac(1, 2, "s")
-        evac(1, 3, "v")
-        evac(1, 4, "s")
-        quant(1, 0, 2)
-        quant(1, 2, 4)
-        quant(1, 4, 5)
-        multiply(0)
-        run_of_two(2, None)
+        def codes(n, engines):
+            for k in range(5):
+                evac(n, k, engines[k])
+            quant(n, 0, 2)
+            quant(n, 2, 4)
+            quant(n, 4, 5)
+
+        def act_planes(g):
+            gelu(g, 0, BATCH)
+            regroup(hpl[:, 4 * g : 4 * g + 4, :], hgrp, g, 0, NPIX)
+
+        new_codes(0)
+        transposes(0, 0, 20)
+        evac(0, 0, "s")
+        evac(0, 1, "s")
+        evac(0, 2, "v")
+        evac(0, 3, "v")
+        evac(0, 4, "v")
+        act_planes(0)
+        quant(0, 0, 2)
+        quant_act(hgrp, hcod, hscl, 0)
+        pt2 = psum.tile([P, 512], F32, name="pt2", tag="acc2")
+        nc.tensor.transpose(pt2[:, 0:P], prw2[:].bitcast(F32), ident[:])
+        act_planes(1)
+        quant(0, 2, 4)
+        quant_act(hgrp, hcod, hscl, 1)
+        act_planes(2)
+        quant(0, 4, 5)
+        quant_act(hgrp, hcod, hscl, 2)
+        bias = const.tile([P, 40], F32, name="bias")
+        nc.vector.tensor_copy(out=bias[:], in_=pt2[:, 0:20].bitcast(BF16))
+        act_planes(3)
+        quant_act(hgrp, hcod, hscl, 3)
+        act_planes(4)
+        quant_act(hgrp, hcod, hscl, 4)
+
+        load_unit(NB)
+        accs = [psum.tile([P, 512], F32, name="acc%d" % e, tag="acc%d" % e) for e in range(2)]
+        for g in range(G - 1):
+            for e in range(2):
+                mx_pass(accs[e][:, 0:256], 0, e, g, hcod, hscl, 0, 256)
+        new_codes(1)
+        transposes(1, 0, 20)
+        for e in range(2):
+            mx_pass(accs[e][:, 0:256], 0, e, G - 1, hcod, hscl, 0, 256)
+        for e in range(2):
+            for g in range(G):
+                mx_pass(accs[e][:, 256:NPIX], 0, e, g, hcod, hscl, 256, NPIX)
+        codes(1, "svsvs")
+        for e in range(2):
+            tile_out(0, e, accs[e])
+        load_unit(NB + 1)
+        prepare(2)
+        codes(2, "svsvs")
         multiply(1)
-        for a in range(4, 2 * UNITS, 2):
-            run_of_two(a, a - 3)
-            multiply(a - 2)
+        prepare(3)
+        codes(3, "svsvs")
+        multiply(2)
+        finish_pillar(1)
+        prepare(4)
+        codes(4, "svsvs")
+        multiply(3)
+        for a in range(5, 2 * UNITS - 1, 2):
+            run_of_two(a, a - 2)
             multiply(a - 1)
+            multiply(a)
+        prepare(2 * UNITS - 1)
+
+        codes(2 * UNITS - 1, "svsvs")
         multiply(2 * UNITS - 2)
         multiply(2 * UNITS - 1)

@@ -60,9 +60,9 @@ def tile_caterpillarblock_a2_3_np5_pa_kernel(
         nc.gpsimd.memset(prw2[:], 0.0)
 
         for r, vec in enumerate([bn1_g, bn1_b, bn1_m, bn1_v]):
-            nc.scalar.dma_start(
-                out=prw1[10 * r : 10 * r + 10, :], in_=vec.rearrange("(r c) -> r c", c=256)
-            )
+            rows = vec.rearrange("(r c) -> r c", c=256)
+            nc.sync.dma_start(out=prw1[10 * r : 10 * r + 8, :], in_=rows[0:8, :])
+            nc.sync.dma_start(out=prw1[10 * r + 8 : 10 * r + 10, :], in_=rows[8:10, :])
 
         raws = {}
 
@@ -345,16 +345,12 @@ def tile_caterpillarblock_a2_3_np5_pa_kernel(
         act_planes(0)
         quant(0, 0, 2)
         quant_act(hgrp, hcod, hscl, 0)
-        pt2 = psum.tile([P, 512], F32, name="pt2", tag="acc2")
-        nc.tensor.transpose(pt2[:, 0:P], prw2[:].bitcast(F32), ident[:])
         act_planes(1)
         quant(0, 2, 4)
         quant_act(hgrp, hcod, hscl, 1)
         act_planes(2)
         quant(0, 4, 5)
         quant_act(hgrp, hcod, hscl, 2)
-        bias = const.tile([P, 40], F32, name="bias")
-        nc.vector.tensor_copy(out=bias[:], in_=pt2[:, 0:20].bitcast(BF16))
         act_planes(3)
         quant_act(hgrp, hcod, hscl, 3)
         act_planes(4)
@@ -367,6 +363,10 @@ def tile_caterpillarblock_a2_3_np5_pa_kernel(
                 mx_pass(accs[e][:, 0:256], 0, e, g, hcod, hscl, 0, 256)
         new_codes(1)
         transposes(1, 0, 20)
+        pt2 = psum.tile([P, 512], F32, name="pt2", tag="acc2")
+        nc.tensor.transpose(pt2[:, 0:P], prw2[:].bitcast(F32), ident[:])
+        bias = const.tile([P, 40], F32, name="bias")
+        nc.vector.tensor_copy(out=bias[:], in_=pt2[:, 0:20].bitcast(BF16))
         for e in range(2):
             mx_pass(accs[e][:, 0:256], 0, e, G - 1, hcod, hscl, 0, 256)
         for e in range(2):

@@ -43,7 +43,7 @@ def tile_caterpillarblock_a2_3_np5_pa_kernel(
         ctx.enter_context(tc.manual_schedule())
 
         ident = const.tile([P, P], F32, name="ident")
-        prw1 = const.tile([P, 256], BF16, name="prw1")
+        prw1 = const.tile([P, 640], F32, name="prw1")
         prw2 = const.tile([P, 256], BF16, name="prw2")
         x_sb = const.tile([P, UNITS, BATCH, 2, PIX], BF16, name="x_sb")
         hpl = const.tile([P, 2 * UNITS, NPIX], BF16, name="hpl")
@@ -60,9 +60,9 @@ def tile_caterpillarblock_a2_3_np5_pa_kernel(
         nc.gpsimd.memset(prw2[:], 0.0)
 
         for r, vec in enumerate([bn1_g, bn1_b, bn1_m, bn1_v]):
-            rows = vec.rearrange("(r c) -> r c", c=256)
-            nc.sync.dma_start(out=prw1[10 * r : 10 * r + 8, :], in_=rows[0:8, :])
-            nc.sync.dma_start(out=prw1[10 * r + 8 : 10 * r + 10, :], in_=rows[8:10, :])
+            nc.sync.dma_start(
+                out=prw1[2 * r : 2 * r + 2, :].bitcast(BF16), in_=vec.rearrange("(h c) -> h c", c=1280)
+            )
 
         raws = {}
 
@@ -113,13 +113,19 @@ def tile_caterpillarblock_a2_3_np5_pa_kernel(
         nc.gpsimd.memset(cpl[1][:], 0.0)
 
         pt1 = psum.tile([P, 512], F32, name="pt1", tag="acc1")
-        nc.tensor.transpose(pt1[:, 0:P], prw1[:].bitcast(F32), ident[:])
+        for i in range(5):
+            nc.tensor.transpose(pt1[:, 96 * i : 96 * i + P], prw1[:, P * i : P * i + P], ident[:])
+        vecs = pt1[:, 0:480].bitcast(BF16).rearrange("p (i j e) -> p i j e", i=5, e=2)
         ve = const.tile([P, 20], F32, name="ve")
-        nc.vector.tensor_scalar_add(out=ve[:], in0=pt1[:, 30:40].bitcast(BF16), scalar1=EPS_BN)
+        nc.vector.tensor_scalar_add(
+            out=ve[:].rearrange("p (h i e) -> p i h e", i=5, e=2), in0=vecs[:, :, 6:8, :], scalar1=EPS_BN
+        )
         sd = const.tile([P, 20], F32, name="sd")
         nc.scalar.activation(out=sd[:], in_=ve[:], func=ACT.Sqrt)
         prm = const.tile([P, 60], F32, name="prm")
-        nc.vector.tensor_copy(out=prm[:], in_=pt1[:, 0:30].bitcast(BF16))
+        nc.vector.tensor_copy(
+            out=prm[:].rearrange("p (j i e) -> p i j e", i=5, e=2), in_=vecs[:, :, 0:6, :]
+        )
         warm = const.tile([P, 1], F32, name="warm")
         nc.scalar.activation(out=warm[:], in_=sd[:, 0:1], func=ACT.Gelu)
         r0 = const.tile([P, 20], F32, name="r0")

@@ -156,9 +156,8 @@ def tile_caterpillarblock_a2_3_np5_pa_kernel(
             rawf = raws[n][:].bitcast(F32)
             for i in range(lo, hi):
                 if i % 4 == 0:
-                    tbs[(n, i // 4)] = psum.tile(
-                        [P, 512], F32, name="tb%d" % (i // 4), tag="tb%d" % (i // 4)
-                    )
+                    b = (5 * n + i // 4) % 6
+                    tbs[(n, i // 4)] = psum.tile([P, 512], F32, name="tb%d" % b, tag="tb%d" % b)
                 nc.tensor.transpose(
                     tbs[(n, i // 4)][:, P * (i % 4) : P * (i % 4) + P],
                     rawf[:, P * i : P * i + P],
@@ -227,7 +226,7 @@ def tile_caterpillarblock_a2_3_np5_pa_kernel(
             )
 
         def products(n, e, cod, scl):
-            m = (2 * n + e) % 3
+            m = e
             acc = psum.tile([P, 512], F32, name="acc%d" % m, tag="acc%d" % m)
             for q0, q1 in ((0, 256), (256, NPIX)):
                 for g in range(G):
@@ -369,7 +368,7 @@ def tile_caterpillarblock_a2_3_np5_pa_kernel(
                 mx_pass(accs[e][:, 0:256], 0, e, g, hcod, hscl, 0, 256)
         new_codes(1)
         transposes(1, 0, 20)
-        pt2 = psum.tile([P, 512], F32, name="pt2", tag="acc2")
+        pt2 = psum.tile([P, 512], F32, name="pt2", tag="tb4")
         nc.tensor.transpose(pt2[:, 0:P], prw2[:].bitcast(F32), ident[:])
         bias = const.tile([P, 40], F32, name="bias")
         nc.vector.tensor_copy(out=bias[:], in_=pt2[:, 0:20].bitcast(BF16))

@@ -340,6 +340,27 @@ def tile_caterpillarblock_a2_3_np5_pa_kernel(
             gelu(g, 0, BATCH)
             regroup(hpl[:, 4 * g : 4 * g + 4, :], hgrp, g, 0, NPIX)
 
+        def even_run_of_two(a):
+            b = a + 1
+            prepare(a)
+            evac(a, 0, "s")
+            evac(a, 1, "v")
+            evac(a, 2, "s")
+            evac(a, 3, "v")
+            evac(a, 4, "s")
+            prepare(b)
+            evac(b, 0, "v")
+            quant(a, 0, 2)
+            evac(b, 1, "s")
+            evac(b, 2, "v")
+            evac(b, 3, "s")
+            evac(b, 4, "v")
+            quant(a, 2, 4)
+            quant(a, 4, 5)
+            quant(b, 0, 2)
+            quant(b, 2, 4)
+            quant(b, 4, 5)
+
         new_codes(0)
         transposes(0, 0, 20)
         evac(0, 0, "s")
@@ -392,7 +413,10 @@ def tile_caterpillarblock_a2_3_np5_pa_kernel(
         codes(4, "svsvs")
         multiply(3)
         for a in range(5, 2 * UNITS - 1, 2):
-            run_of_two(a, a - 2)
+            if a <= UNITS + 1:
+                run_of_two(a, a - 2)
+            else:
+                even_run_of_two(a)
             multiply(a - 1)
             multiply(a)
         prepare(2 * UNITS - 1)

@@ -50,14 +50,23 @@ def tile_caterpillarblock_a2_3_np5_pa_kernel(
         hgrp = const.tile([P, G, NPIX, 4], BF16, name="hgrp", align_bytes=64)
         hcod = const.tile([P, G, NPIX], U32, name="hcod", align_bytes=64)
         hscl = const.tile([P, G, NPIX], U8, name="hscl", align_bytes=64)
-        cpl = [const.tile([P, 4, NPIX], BF16, name="cpl%d" % i) for i in range(2)]
+        cpl = [const.tile([P, 4, NPIX], BF16, name="cpl%d" % i) for i in range(5)]
         cgrp = const.tile([P, G, NPIX, 4], BF16, name="cgrp", align_bytes=64)
         ccod = const.tile([P, G, NPIX], U32, name="ccod", align_bytes=64)
         cscl = const.tile([P, G, NPIX], U8, name="cscl", align_bytes=64)
 
         nc.vector.memset(prw1[:], 0.0)
+        for pil in range(4):
+            nc.vector.memset(cpl[pil][:], 0.0)
         make_identity(nc, ident[:])
         nc.gpsimd.memset(prw2[:], 0.0)
+
+        used = []
+
+        def next_bank():
+            b = len(used) % 8
+            used.append(b)
+            return psum.tile([P, 512], F32, name="bank%d" % b, tag="bank%d" % b)
 
         for r, vec in enumerate([bn1_g, bn1_b, bn1_m, bn1_v]):
             nc.sync.dma_start(
@@ -109,10 +118,8 @@ def tile_caterpillarblock_a2_3_np5_pa_kernel(
                 out=prw2[2 * r : 2 * r + 2, :], in_=vec.rearrange("(r c) -> r c", c=256)
             )
         nc.gpsimd.dma_start(out=prw2[10:20, :], in_=bf1.rearrange("(r c) -> r c", c=256))
-        nc.gpsimd.memset(cpl[0][:], 0.0)
-        nc.gpsimd.memset(cpl[1][:], 0.0)
 
-        pt1 = psum.tile([P, 512], F32, name="pt1", tag="acc1")
+        pt1 = next_bank()
         for i in range(5):
             nc.tensor.transpose(pt1[:, 96 * i : 96 * i + P], prw1[:, P * i : P * i + P], ident[:])
         vecs = pt1[:, 0:480].bitcast(BF16).rearrange("p (i j e) -> p i j e", i=5, e=2)
@@ -156,8 +163,7 @@ def tile_caterpillarblock_a2_3_np5_pa_kernel(
             rawf = raws[n][:].bitcast(F32)
             for i in range(lo, hi):
                 if i % 4 == 0:
-                    b = (5 * n + i // 4) % 6
-                    tbs[(n, i // 4)] = psum.tile([P, 512], F32, name="tb%d" % b, tag="tb%d" % b)
+                    tbs[(n, i // 4)] = next_bank()
                 nc.tensor.transpose(
                     tbs[(n, i // 4)][:, P * (i % 4) : P * (i % 4) + P],
                     rawf[:, P * i : P * i + P],
@@ -226,8 +232,7 @@ def tile_caterpillarblock_a2_3_np5_pa_kernel(
             )
 
         def products(n, e, cod, scl):
-            m = e
-            acc = psum.tile([P, 512], F32, name="acc%d" % m, tag="acc%d" % m)
+            acc = next_bank()
             for q0, q1 in ((0, 256), (256, NPIX)):
                 for g in range(G):
                     mx_pass(acc[:, q0:q1], n, e, g, cod, scl, q0, q1)
@@ -241,13 +246,19 @@ def tile_caterpillarblock_a2_3_np5_pa_kernel(
         def tile_out(n, e, acc):
             if n < UNITS:
                 pil, u = n // 2, n % 2
-                d = SHIFT[pil]
-                lo = max(0, -d)
-                hi = min(NPIX, NPIX - d)
                 t = 2 * u + e
+                d = SHIFT[pil]
+                dst = cpl[pil][:, t, :]
+                src = acc[:, 0:NPIX]
+                run, step = (12, 1) if abs(d) == 1 else (PIX, abs(d))
+                if d != 0:
+                    keep = slice(0, run - step)
+                    move = slice(step, run)
+                    dst = dst.rearrange("p (n j) -> p n j", j=run)[:, :, keep if d < 0 else move]
+                    src = src.rearrange("p (n j) -> p n j", j=run)[:, :, move if d < 0 else keep]
                 nc.scalar.activation(
-                    out=cpl[pil % 2][:, t, lo + d : hi + d],
-                    in_=acc[:, lo:hi],
+                    out=dst,
+                    in_=src,
                     func=ACT.Identity,
                     bias=bias[:, 4 * pil + t : 4 * pil + t + 1],
                     scale=1.0,
@@ -278,22 +289,8 @@ def tile_caterpillarblock_a2_3_np5_pa_kernel(
                     in_=osb[:].rearrange("p b e q -> p b (e q)"),
                 )
 
-        def finish_pillar(n):
-            if n >= UNITS or n % 2 == 0:
-                return
-            pil = n // 2
-            d = SHIFT[pil]
-            regroup(cpl[pil % 2], cgrp, pil, 0, NPIX)
-            by_image = cgrp[:, pil, :, :].rearrange("p (b r) t -> p b (r t)", b=BATCH)
-            by_row = cgrp[:, pil, :, :].rearrange("p (n j) t -> p n (j t)", j=12)
-            if d == -12:
-                nc.vector.memset(by_image[:, :, 84 * 4 : 96 * 4], 0.0)
-            elif d == 12:
-                nc.vector.memset(by_image[:, :, 0 : 12 * 4], 0.0)
-            elif d == 1:
-                nc.vector.memset(by_row[:, :, 0:4], 0.0)
-            elif d == -1:
-                nc.vector.memset(by_row[:, :, 44:48], 0.0)
+        def finish_pillar(pil):
+            regroup(cpl[pil], cgrp, pil, 0, NPIX)
             quant_act(cgrp, ccod, cscl, pil)
 
         def multiply(n):
@@ -306,60 +303,28 @@ def tile_caterpillarblock_a2_3_np5_pa_kernel(
             if n + NB < 2 * UNITS:
                 load_unit(n + NB)
 
-        def run_of_two(a, pending):
-            b = a + 1
-            prepare(a)
-            evac(a, 0, "s")
-            evac(a, 1, "v")
-            evac(a, 2, "s")
-            evac(a, 3, "v")
-            evac(a, 4, "s")
-            prepare(b)
-            if pending is not None:
-                finish_pillar(pending)
-            quant(a, 0, 2)
-            evac(b, 0, "s")
-            evac(b, 1, "s")
-            evac(b, 2, "v")
-            evac(b, 3, "s")
-            evac(b, 4, "s")
-            quant(a, 2, 4)
-            quant(a, 4, 5)
-            quant(b, 0, 2)
-            quant(b, 2, 4)
-            quant(b, 4, 5)
-
-        def codes(n, engines):
-            for k in range(5):
-                evac(n, k, engines[k])
-            quant(n, 0, 2)
-            quant(n, 2, 4)
+        def codes(n):
+            quant(n, 0, 4)
             quant(n, 4, 5)
+
+        def run(units, engines, early=None, pillar=None, late_pillar=None):
+            for n, split in zip(units, engines):
+                prepare(n)
+                for k in range(5):
+                    evac(n, k, split[k])
+                if n == early:
+                    codes(n)
+                if n == units[0] and pillar is not None:
+                    finish_pillar(pillar)
+            if late_pillar is not None:
+                finish_pillar(late_pillar)
+            for n in units:
+                if n != early:
+                    codes(n)
 
         def act_planes(g):
             gelu(g, 0, BATCH)
             regroup(hpl[:, 4 * g : 4 * g + 4, :], hgrp, g, 0, NPIX)
-
-        def even_run_of_two(a):
-            b = a + 1
-            prepare(a)
-            evac(a, 0, "s")
-            evac(a, 1, "v")
-            evac(a, 2, "s")
-            evac(a, 3, "v")
-            evac(a, 4, "s")
-            prepare(b)
-            evac(b, 0, "v")
-            quant(a, 0, 2)
-            evac(b, 1, "s")
-            evac(b, 2, "v")
-            evac(b, 3, "s")
-            evac(b, 4, "v")
-            quant(a, 2, 4)
-            quant(a, 4, 5)
-            quant(b, 0, 2)
-            quant(b, 2, 4)
-            quant(b, 4, 5)
 
         new_codes(0)
         transposes(0, 0, 20)
@@ -383,13 +348,13 @@ def tile_caterpillarblock_a2_3_np5_pa_kernel(
         quant_act(hgrp, hcod, hscl, 4)
 
         load_unit(NB)
-        accs = [psum.tile([P, 512], F32, name="acc%d" % e, tag="acc%d" % e) for e in range(2)]
+        pt2 = next_bank()
+        accs = [next_bank() for e in range(2)]
         for g in range(G - 1):
             for e in range(2):
                 mx_pass(accs[e][:, 0:256], 0, e, g, hcod, hscl, 0, 256)
         new_codes(1)
         transposes(1, 0, 20)
-        pt2 = psum.tile([P, 512], F32, name="pt2", tag="tb4")
         nc.tensor.transpose(pt2[:, 0:P], prw2[:].bitcast(F32), ident[:])
         bias = const.tile([P, 40], F32, name="bias")
         nc.vector.tensor_copy(out=bias[:], in_=pt2[:, 0:20].bitcast(BF16))
@@ -398,29 +363,33 @@ def tile_caterpillarblock_a2_3_np5_pa_kernel(
         for e in range(2):
             for g in range(G):
                 mx_pass(accs[e][:, 256:NPIX], 0, e, g, hcod, hscl, 256, NPIX)
-        codes(1, "svsvs")
+        for k in range(5):
+            evac(1, k, "svsvs"[k])
+        codes(1)
         for e in range(2):
             tile_out(0, e, accs[e])
         load_unit(NB + 1)
-        prepare(2)
-        codes(2, "svsvs")
+        run((2,), ("svsvs",))
         multiply(1)
-        prepare(3)
-        codes(3, "svsvs")
+        run((3,), ("svsvs",), late_pillar=0)
         multiply(2)
-        finish_pillar(1)
-        prepare(4)
-        codes(4, "svsvs")
+        run((4,), ("svsvs",))
         multiply(3)
-        for a in range(5, 2 * UNITS - 1, 2):
-            if a <= UNITS + 1:
-                run_of_two(a, a - 2)
-            else:
-                even_run_of_two(a)
+        run((5, 6), ("svsvs", "vsvss"), early=5, late_pillar=1)
+        multiply(4)
+        multiply(5)
+        run((7, 8, 9), ("svsvs", "svsvs", "svsvs"), early=7, late_pillar=2)
+        multiply(6)
+        multiply(7)
+        run((10, 11), ("svsvs", "vsvss"), late_pillar=3)
+        multiply(8)
+        multiply(9)
+        run((12, 13), ("svsvs", "vsvsv"), pillar=4)
+        multiply(10)
+        multiply(11)
+        for a in range(14, 2 * UNITS, 2):
+            run((a, a + 1), ("svsvs", "vsvsv"))
+            multiply(a - 2)
             multiply(a - 1)
-            multiply(a)
-        prepare(2 * UNITS - 1)
-
-        codes(2 * UNITS - 1, "svsvs")
         multiply(2 * UNITS - 2)
         multiply(2 * UNITS - 1)

@@ -57,7 +57,10 @@ def tile_caterpillarblock_a2_3_np5_pa_kernel(
 
         nc.vector.memset(prw1[:], 0.0)
         for pil in range(4):
-            nc.vector.memset(cpl[pil][:], 0.0)
+            d = SHIFT[pil]
+            run, step = (12, 2) if abs(d) == 1 else (PIX, abs(d))
+            edge = slice(run - step, run) if d < 0 else slice(0, step)
+            nc.vector.memset(cpl[pil][:].rearrange("p t (n j) -> p t n j", j=run)[:, :, :, edge], 0.0)
         make_identity(nc, ident[:])
         nc.gpsimd.memset(prw2[:], 0.0)
 
@@ -276,18 +279,31 @@ def tile_caterpillarblock_a2_3_np5_pa_kernel(
                 bias=bias[:, col : col + 1],
                 scale=1.0,
             )
-            if n == 2 * UNITS - 1:
-                nc.sync.dma_start(
-                    out=outv[:, 256 * uo : 256 * uo + 256, :].rearrange("b (p e) q -> p e b q", e=2)[
-                        :, e, :, :
-                    ],
-                    in_=osb[:, :, e, :],
-                )
-            elif e == 1:
+            if e == 1:
                 nc.sync.dma_start(
                     out=outv[:, 256 * uo : 256 * uo + 256, :].rearrange("b (p e) q -> p b (e q)", e=2),
                     in_=osb[:].rearrange("p b e q -> p b (e q)"),
                 )
+
+        def last_unit():
+            n = 2 * UNITS - 1
+            rows = outv[:, C - 256 : C, :].rearrange("b (p e) q -> p e b q", e=2)
+            for e in range(2):
+                tile_sb = outp.tile([P, NPIX], F32, name="last", tag="last")
+                images = tile_sb[:].rearrange("p (b q) -> p b q", b=BATCH)
+                col = 20 + 2 * (n - UNITS) + e
+                for q0, q1, b0, b1 in ((0, 256, 0, 2), (256, NPIX, 2, BATCH)):
+                    acc = next_bank()
+                    for g in range(G):
+                        mx_pass(acc[:, 0 : q1 - q0], n, e, g, ccod, cscl, q0, q1)
+                    nc.scalar.activation(
+                        out=tile_sb[:, q0:q1],
+                        in_=acc[:, 0 : q1 - q0],
+                        func=ACT.Identity,
+                        bias=bias[:, col : col + 1],
+                        scale=1.0,
+                    )
+                    nc.sync.dma_start(out=rows[:, e, b0:b1, :], in_=images[:, b0:b1, :])
 
         def finish_pillar(pil):
             regroup(cpl[pil], cgrp, pil, 0, NPIX)
@@ -392,4 +408,4 @@ def tile_caterpillarblock_a2_3_np5_pa_kernel(
             multiply(a - 2)
             multiply(a - 1)
         multiply(2 * UNITS - 2)
-        multiply(2 * UNITS - 1)
+        last_unit()

@@ -349,28 +349,37 @@ def tile_caterpillarblock_a2_3_np5_pa_kernel(
         evac(0, 2, "v")
         evac(0, 3, "v")
         evac(0, 4, "v")
-        act_planes(0)
         quant(0, 0, 2)
+        act_planes(0)
+        quant(0, 2, 4)
         quant_act(hgrp, hcod, hscl, 0)
         act_planes(1)
-        quant(0, 2, 4)
+        quant(0, 4, 5)
         quant_act(hgrp, hcod, hscl, 1)
         act_planes(2)
-        quant(0, 4, 5)
         quant_act(hgrp, hcod, hscl, 2)
         act_planes(3)
         quant_act(hgrp, hcod, hscl, 3)
-        act_planes(4)
-        quant_act(hgrp, hcod, hscl, 4)
+        last = hpl[:, 16:20, :]
+        gelu(4, 0, 3)
+        regroup(last, hgrp, 4, 0, 256)
+        gelu(4, 3, BATCH)
+        quant_part(hgrp, hcod, hscl, 4, 0, 256)
+        regroup(last, hgrp, 4, 256, NPIX)
+        quant_part(hgrp, hcod, hscl, 4, 256, NPIX)
 
         load_unit(NB)
         pt2 = next_bank()
         accs = [next_bank() for e in range(2)]
+        new_codes(1)
         for g in range(G - 1):
+            if g == 3:
+                transposes(1, 0, 10)
+            if g == 4:
+                transposes(1, 10, 20)
             for e in range(2):
                 mx_pass(accs[e][:, 0:256], 0, e, g, hcod, hscl, 0, 256)
-        new_codes(1)
-        transposes(1, 0, 20)
+        transposes(1, 10, 20)
         nc.tensor.transpose(pt2[:, 0:P], prw2[:].bitcast(F32), ident[:])
         bias = const.tile([P, 40], F32, name="bias")
         nc.vector.tensor_copy(out=bias[:], in_=pt2[:, 0:20].bitcast(BF16))
@@ -391,13 +400,13 @@ def tile_caterpillarblock_a2_3_np5_pa_kernel(
         multiply(2)
         run((4,), ("svsvs",))
         multiply(3)
-        run((5, 6), ("svsvs", "vsvss"), early=5, late_pillar=1)
+        run((5, 6), ("svsvs", "ssvss"), early=5, late_pillar=1)
         multiply(4)
         multiply(5)
-        run((7, 8, 9), ("svsvs", "svsvs", "svsvs"), early=7, late_pillar=2)
+        run((7, 8, 9), ("svsvs", "ssvss", "svsvs"), early=7, late_pillar=2)
         multiply(6)
         multiply(7)
-        run((10, 11), ("svsvs", "vsvss"), late_pillar=3)
+        run((10, 11), ("svsvs", "ssvss"), late_pillar=3)
         multiply(8)
         multiply(9)
         run((12, 13), ("svsvs", "vsvsv"), pillar=4)

from contextlib import ExitStack

import concourse.mybir as mybir
from concourse.masks import make_identity

F32 = mybir.dt.float32
BF16 = mybir.dt.bfloat16
U32 = mybir.dt.uint32
U8 = mybir.dt.uint8
FP8X4 = mybir.dt.float8_e4m3fn_x4
ACT = mybir.ActivationFunctionType
ALU = mybir.AluOpType

P = 128
BATCH = 4
C = 2560
PIX = 96
NPIX = BATCH * PIX
G = 5
UNITS = 10
NB = 7
EPS_BN = 1e-5
SHIFT = [-12, 12, 1, -1, 0]

FLOPS = 2 * 2 * C * C * NPIX


def tile_caterpillarblock_a2_3_np5_pa_kernel(
    tc, x, bn1_g, bn1_b, bn1_m, bn1_v, wt, bt, wb, bb, wr, br, wl, bl, wc, bc, wf1, bf1, out
):
    nc = tc.nc
    pillars = [wt, wb, wr, wl, wc]
    xv = x.rearrange("b c i j -> b c (i j)")
    outv = out.rearrange("b c i j -> b c (i j)")

    with ExitStack() as ctx:
        const = ctx.enter_context(tc.tile_pool(name="const", bufs=1))
        rawp = ctx.enter_context(tc.tile_pool(name="rawp", bufs=NB))
        grpp = ctx.enter_context(tc.tile_pool(name="grpp", bufs=3))
        codp = ctx.enter_context(tc.tile_pool(name="codp", bufs=4))
        outp = ctx.enter_context(tc.tile_pool(name="outp", bufs=3))
        psum = ctx.enter_context(tc.psum_pool(name="psum", bufs=1))
        ctx.enter_context(tc.manual_schedule())

        ident = const.tile([P, P], F32, name="ident")
        prw1 = const.tile([P, 640], F32, name="prw1")
        prw2 = const.tile([P, 256], BF16, name="prw2")
        x_sb = const.tile([P, UNITS, BATCH, 2, PIX], BF16, name="x_sb")
        hpl = const.tile([P, 2 * UNITS, NPIX], BF16, name="hpl")
        hgrp = const.tile([P, G, NPIX, 4], BF16, name="hgrp", align_bytes=64)
        hcod = const.tile([P, G, NPIX], U32, name="hcod", align_bytes=64)
        hscl = const.tile([P, G, NPIX], U8, name="hscl", align_bytes=64)
        cpl = [const.tile([P, 4, NPIX], BF16, name="cpl%d" % i) for i in range(5)]
        cgrp = const.tile([P, G, NPIX, 4], BF16, name="cgrp", align_bytes=64)
        ccod = const.tile([P, G, NPIX], U32, name="ccod", align_bytes=64)
        cscl = const.tile([P, G, NPIX], U8, name="cscl", align_bytes=64)

        nc.vector.memset(prw1[:], 0.0)
        for pil in range(4):
            d = SHIFT[pil]
            run, step = (12, 2) if abs(d) == 1 else (PIX, abs(d))
            edge = slice(run - step, run) if d < 0 else slice(0, step)
            nc.vector.memset(cpl[pil][:].rearrange("p t (n j) -> p t n j", j=run)[:, :, :, edge], 0.0)
        make_identity(nc, ident[:])
        nc.gpsimd.memset(prw2[:], 0.0)

        used = []

        def next_bank():
            b = len(used) % 8
            used.append(b)
            return psum.tile([P, 512], F32, name="bank%d" % b, tag="bank%d" % b)

        for r, vec in enumerate([bn1_g, bn1_b, bn1_m, bn1_v]):
            nc.sync.dma_start(
                out=prw1[2 * r : 2 * r + 2, :].bitcast(BF16), in_=vec.rearrange("(h c) -> h c", c=1280)
            )

        raws = {}

        def unit_rows(n):
            if n < UNITS:
                return pillars[n // 2][256 * (n % 2) : 256 * (n % 2) + 256, :]
            return wf1[256 * (n - UNITS) : 256 * (n - UNITS) + 256, :]

        def new_raw(n):
            raws[n] = rawp.tile([P, 2 * C], BF16, name="wraw", tag="wraw")

        def load_half(n, e):
            nc.sync.dma_start(
                out=raws[n][:, e * C : (e + 1) * C],
                in_=unit_rows(n).rearrange("(p e) c -> p e c", e=2)[:, e, :],
            )

        def load_unit(n):
            new_raw(n)
            nc.sync.dma_start(out=raws[n][:], in_=unit_rows(n).rearrange("(p e) c -> p (e c)", e=2))

        def load_x(u):
            nc.sync.dma_start(
                out=x_sb[:, u, :, :, :].rearrange("p b e q -> p b (e q)"),
                in_=xv[:, 256 * u : 256 * u + 256, :].rearrange("b (p e) q -> p b (e q)", e=2),
            )

        def load_halves(n):
            new_raw(n)
            load_half(n, 0)
            load_half(n, 1)

        load_halves(0)
        for u in range(UNITS):
            load_x(u)
        load_halves(1)
        load_halves(2)
        load_halves(3)
        for n in range(4, NB):
            load_unit(n)

        for r, vec in enumerate([bt, bb, br, bl, bc]):
            nc.gpsimd.dma_start(
                out=prw2[2 * r : 2 * r + 2, :], in_=vec.rearrange("(r c) -> r c", c=256)
            )
        nc.gpsimd.dma_start(out=prw2[10:20, :], in_=bf1.rearrange("(r c) -> r c", c=256))

        pt1 = next_bank()
        for i in range(5):
            nc.tensor.transpose(pt1[:, 96 * i : 96 * i + P], prw1[:, P * i : P * i + P], ident[:])
        vecs = pt1[:, 0:480].bitcast(BF16).rearrange("p (i j e) -> p i j e", i=5, e=2)
        ve = const.tile([P, 20], F32, name="ve")
        nc.vector.tensor_scalar_add(
            out=ve[:].rearrange("p (h i e) -> p i h e", i=5, e=2), in0=vecs[:, :, 6:8, :], scalar1=EPS_BN
        )
        sd = const.tile([P, 20], F32, name="sd")
        nc.scalar.activation(out=sd[:], in_=ve[:], func=ACT.Sqrt)
        prm = const.tile([P, 60], F32, name="prm")
        nc.vector.tensor_copy(
            out=prm[:].rearrange("p (j i e) -> p i j e", i=5, e=2), in_=vecs[:, :, 0:6, :]
        )
        warm = const.tile([P, 1], F32, name="warm")
        nc.scalar.activation(out=warm[:], in_=sd[:, 0:1], func=ACT.Gelu)
        r0 = const.tile([P, 20], F32, name="r0")
        nc.vector.reciprocal(out=r0[:], in_=sd[:])
        na = const.tile([P, 20], F32, name="na")
        nb = const.tile([P, 20], F32, name="nb")
        rg = const.tile([P, 20], F32, name="rg")
        nc.vector.scalar_tensor_tensor(
            out=na[:], in0=r0[:], scalar=-0.5, in1=ve[:], op0=ALU.mult, op1=ALU.mult
        )
        nc.vector.tensor_mul(out=rg[:], in0=r0[:], in1=prm[:, 0:20])
        nc.vector.tensor_mul(out=nb[:], in0=na[:], in1=r0[:])
        bn_s = const.tile([P, 20], F32, name="bn_s")
        bn_o = const.tile([P, 20], F32, name="bn_o")
        ms = const.tile([P, 20], F32, name="ms")
        nc.vector.scalar_tensor_tensor(
            out=bn_s[:], in0=nb[:], scalar=1.5, in1=rg[:], op0=ALU.add, op1=ALU.mult
        )
        nc.vector.tensor_mul(out=ms[:], in0=bn_s[:], in1=prm[:, 40:60])
        nc.vector.tensor_sub(out=bn_o[:], in0=prm[:, 20:40], in1=ms[:])

        tbs = {}
        wgrps = {}
        wcods = {}
        wscls = {}

        def transposes(n, lo, hi):
            rawf = raws[n][:].bitcast(F32)
            for i in range(lo, hi):
                if i % 4 == 0:
                    tbs[(n, i // 4)] = next_bank()
                nc.tensor.transpose(
                    tbs[(n, i // 4)][:, P * (i % 4) : P * (i % 4) + P],
                    rawf[:, P * i : P * i + P],
                    ident[:],
                )

        def new_codes(n):
            wgrps[n] = grpp.tile([P, 2 * C], BF16, name="wgrp", tag="wgrp", align_bytes=64)
            wcods[n] = codp.tile([P, 10 * P], U32, name="wcod", tag="wcod", align_bytes=64)
            wscls[n] = codp.tile([P, 10 * P], U8, name="wscl", tag="wscl", align_bytes=64)

        def evac(n, k, eng):
            dst = wgrps[n][:].bitcast(F32)[:, 512 * k : 512 * k + 512].rearrange(
                "p (n o u) -> p n o u", n=2, u=2
            )
            src = tbs[(n, k)][:].rearrange("p (n u o) -> p n o u", n=2, u=2)
            if eng == "v":
                nc.vector.tensor_copy(out=dst, in_=src)
            else:
                nc.scalar.copy(out=dst, in_=src)

        def quant(n, k0, k1):
            nc.vector.quantize_mx(
                out=wcods[n][:, 256 * k0 : 256 * k1].bitcast(FP8X4),
                scales=wscls[n][:, 256 * k0 : 256 * k1],
                in_=wgrps[n][:, 1024 * k0 : 1024 * k1],
            )

        def gelu(g, b0, b1):
            for col in range(4 * g, 4 * g + 4):
                nc.scalar.activation(
                    out=hpl[:, col, PIX * b0 : PIX * b1].rearrange("p (b q) -> p b q", q=PIX),
                    in_=x_sb[:, col // 2, b0:b1, col % 2, :],
                    func=ACT.Gelu,
                    bias=bn_o[:, col : col + 1],
                    scale=bn_s[:, col : col + 1],
                )

        def regroup(planes, grp, g, q0, q1):
            nc.vector.tensor_copy(
                out=grp[:, g, q0:q1, :].rearrange("p (c i) t -> p c t i", i=4),
                in_=planes[:, :, q0:q1].rearrange("p t (c i) -> p c t i", i=4),
            )

        def quant_part(grp, cod, scl, g, q0, q1):
            nc.vector.quantize_mx(
                out=cod[:, g, q0:q1].bitcast(FP8X4),
                scales=scl[:, g, q0:q1],
                in_=grp[:, g, q0:q1, :].rearrange("p q t -> p (q t)"),
            )

        def quant_act(grp, cod, scl, g):
            quant_part(grp, cod, scl, g, 0, 256)
            quant_part(grp, cod, scl, g, 256, NPIX)

        def mx_pass(acc_ap, n, e, g, cod, scl, q0, q1):
            w0 = P * (G * e + g)
            nc.tensor.matmul_mx(
                out=acc_ap,
                lhsT=wcods[n][:, w0 : w0 + P].bitcast(FP8X4),
                lhsT_scale=wscls[n][:, w0 : w0 + P],
                rhs=cod[:, g, q0:q1].bitcast(FP8X4),
                rhs_scale=scl[:, g, q0:q1],
                start=(g == 0),
                stop=(g == G - 1),
            )

        def products(n, e, cod, scl):
            acc = next_bank()
            for q0, q1 in ((0, 256), (256, NPIX)):
                for g in range(G):
                    mx_pass(acc[:, q0:q1], n, e, g, cod, scl, q0, q1)
            return acc

        osbs = {}

        def tile_products(n, e):
            tile_out(n, e, products(n, e, hcod, hscl) if n < UNITS else products(n, e, ccod, cscl))

        def tile_out(n, e, acc):
            if n < UNITS:
                pil, u = n // 2, n % 2
                t = 2 * u + e
                d = SHIFT[pil]
                dst = cpl[pil][:, t, :]
                src = acc[:, 0:NPIX]
                run, step = (12, 1) if abs(d) == 1 else (PIX, abs(d))
                if d != 0:
                    keep = slice(0, run - step)
                    move = slice(step, run)
                    dst = dst.rearrange("p (n j) -> p n j", j=run)[:, :, keep if d < 0 else move]
                    src = src.rearrange("p (n j) -> p n j", j=run)[:, :, move if d < 0 else keep]
                nc.scalar.activation(
                    out=dst,
                    in_=src,
                    func=ACT.Identity,
                    bias=bias[:, 4 * pil + t : 4 * pil + t + 1],
                    scale=1.0,
                )
                return
            uo = n - UNITS
            if e == 0:
                osbs[n] = outp.tile([P, BATCH, 2, PIX], F32, name="osb", tag="osb")
            osb = osbs[n]
            col = 20 + 2 * uo + e
            nc.scalar.activation(
                out=osb[:, :, e, :],
                in_=acc[:, 0:NPIX].rearrange("p (b q) -> p b q", b=BATCH),
                func=ACT.Identity,
                bias=bias[:, col : col + 1],
                scale=1.0,
            )
            if e == 1:
                nc.sync.dma_start(
                    out=outv[:, 256 * uo : 256 * uo + 256, :].rearrange("b (p e) q -> p b (e q)", e=2),
                    in_=osb[:].rearrange("p b e q -> p b (e q)"),
                )

        def last_unit():
            n = 2 * UNITS - 1
            rows = outv[:, C - 256 : C, :].rearrange("b (p e) q -> p e b q", e=2)
            for e in range(2):
                tile_sb = outp.tile([P, NPIX], F32, name="last", tag="last")
                images = tile_sb[:].rearrange("p (b q) -> p b q", b=BATCH)
                col = 20 + 2 * (n - UNITS) + e
                for q0, q1, b0, b1 in ((0, 256, 0, 2), (256, NPIX, 2, BATCH)):
                    acc = next_bank()
                    for g in range(G):
                        mx_pass(acc[:, 0 : q1 - q0], n, e, g, ccod, cscl, q0, q1)
                    nc.scalar.activation(
                        out=tile_sb[:, q0:q1],
                        in_=acc[:, 0 : q1 - q0],
                        func=ACT.Identity,
                        bias=bias[:, col : col + 1],
                        scale=1.0,
                    )
                    nc.sync.dma_start(out=rows[:, e, b0:b1, :], in_=images[:, b0:b1, :])

        def finish_pillar(pil):
            regroup(cpl[pil], cgrp, pil, 0, NPIX)
            quant_act(cgrp, ccod, cscl, pil)

        def multiply(n):
            tile_products(n, 0)
            tile_products(n, 1)

        def prepare(n):
            new_codes(n)
            transposes(n, 0, 20)
            if n + NB < 2 * UNITS:
                load_unit(n + NB)

        def codes(n):
            quant(n, 0, 4)
            quant(n, 4, 5)

        def run(units, engines, early=None, pillar=None, late_pillar=None):
            for n, split in zip(units, engines):
                prepare(n)
                for k in range(5):
                    evac(n, k, split[k])
                if n == early:
                    codes(n)
                if n == units[0] and pillar is not None:
                    finish_pillar(pillar)
            if late_pillar is not None:
                finish_pillar(late_pillar)
            for n in units:
                if n != early:
                    codes(n)

        def act_planes(g):
            gelu(g, 0, BATCH)
            regroup(hpl[:, 4 * g : 4 * g + 4, :], hgrp, g, 0, NPIX)

        new_codes(0)
        transposes(0, 0, 20)
        evac(0, 0, "s")
        evac(0, 1, "s")
        evac(0, 2, "v")
        evac(0, 3, "v")
        evac(0, 4, "v")
        quant(0, 0, 2)
        act_planes(0)
        quant(0, 2, 4)
        quant_act(hgrp, hcod, hscl, 0)
        act_planes(1)
        quant(0, 4, 5)
        quant_act(hgrp, hcod, hscl, 1)
        act_planes(2)
        quant_act(hgrp, hcod, hscl, 2)
        act_planes(3)
        quant_act(hgrp, hcod, hscl, 3)
        last = hpl[:, 16:20, :]
        gelu(4, 0, 3)
        regroup(last, hgrp, 4, 0, 256)
        gelu(4, 3, BATCH)
        quant_part(hgrp, hcod, hscl, 4, 0, 256)
        regroup(last, hgrp, 4, 256, NPIX)
        quant_part(hgrp, hcod, hscl, 4, 256, NPIX)

        load_unit(NB)
        pt2 = next_bank()
        accs = [next_bank() for e in range(2)]
        new_codes(1)
        for g in range(G - 1):
            if g == 3:
                transposes(1, 0, 10)
            if g == 4:
                transposes(1, 10, 20)
            for e in range(2):
                mx_pass(accs[e][:, 0:256], 0, e, g, hcod, hscl, 0, 256)
        transposes(1, 10, 20)
        nc.tensor.transpose(pt2[:, 0:P], prw2[:].bitcast(F32), ident[:])
        bias = const.tile([P, 40], F32, name="bias")
        nc.vector.tensor_copy(out=bias[:], in_=pt2[:, 0:20].bitcast(BF16))
        for e in range(2):
            mx_pass(accs[e][:, 0:256], 0, e, G - 1, hcod, hscl, 0, 256)
        for e in range(2):
            for g in range(G):
                mx_pass(accs[e][:, 256:NPIX], 0, e, g, hcod, hscl, 256, NPIX)
        for k in range(5):
            evac(1, k, "svsvs"[k])
        codes(1)
        for e in range(2):
            tile_out(0, e, accs[e])
        load_unit(NB + 1)
        run((2,), ("svsvs",))
        multiply(1)
        run((3,), ("svsvs",), late_pillar=0)
        multiply(2)
        run((4,), ("svsvs",))
        multiply(3)
        run((5, 6), ("svsvs", "ssvss"), early=5, late_pillar=1)
        multiply(4)
        multiply(5)
        run((7, 8, 9), ("svsvs", "ssvss", "svsvs"), early=7, late_pillar=2)
        multiply(6)
        multiply(7)
        run((10, 11), ("svsvs", "ssvss"), late_pillar=3)
        multiply(8)
        multiply(9)
        run((12, 13), ("svsvs", "vsvsv"), pillar=4)
        multiply(10)
        multiply(11)
        for a in range(14, 2 * UNITS, 2):
            run((a, a + 1), ("svsvs", "vsvsv"))
            multiply(a - 2)
            multiply(a - 1)
        multiply(2 * UNITS - 2)
        last_unit()
